import numpy as np
import ml_dtypes


def mxq(x, axis, fmt="e4m3"):
    dtype, down = {"e4m3": (ml_dtypes.float8_e4m3fn, 7), "e5m2": (ml_dtypes.float8_e5m2, 14)}[fmt]
    v = np.moveaxis(np.asarray(x, np.float32).astype(ml_dtypes.bfloat16).astype(np.float64), axis, -1)
    blocks = v.reshape(v.shape[:-1] + (-1, 32))
    amax = np.abs(blocks).max(-1, keepdims=True)
    byte = np.maximum(np.where(amax > 0, np.frexp(amax)[1] - 1 + 127, 0) - down, 1)
    scale = np.exp2(byte - 127.0)
    codes = (blocks / scale).astype(np.float32).astype(dtype).astype(np.float64)
    return np.moveaxis((codes * scale).reshape(v.shape), -1, axis)


WIDE = False


def mx_kscale(k):
    if not WIDE:
        return np.ones(k)
    levels = np.array([10, -10, 5, -5, 0])
    a = np.random.permutation(np.resize(levels, k // 512 * 4)).reshape(k // 512, 4)
    idx = np.arange(k)
    return np.exp2(a[idx // 512, idx % 128 // 32])


BF16 = ml_dtypes.bfloat16


def bf(x):
    return np.asarray(x, np.float32).astype(BF16)


def f64(x):
    return np.asarray(x).astype(np.float64)


B, S, D, F, F2 = 4, 256, 512, 2048, 1024


def erf(v):
    v = np.clip(v, -6.0, 6.0)
    v2 = 2.0 * v * v
    term = v.copy()
    tot = v.copy()
    for n in range(1, 110):
        term = term * v2 / (2.0 * n + 1.0)
        tot = tot + term
    return 2.0 / np.sqrt(np.pi) * np.exp(-v * v) * tot


def gelu(v):
    return 0.5 * v * (1.0 + erf(v / np.sqrt(2.0)))


def sigmoid(v):
    return 1.0 / (1.0 + np.exp(-v))


def setup_inputs():
    n = np.random.standard_normal
    s, t = mx_kscale(D), mx_kscale(D)
    wg = 0.5 / np.sqrt(D)
    wu = 1.5 / np.sqrt(D)
    return {'amp': bf(np.abs(n((B, S, D))) * 1.5 * s),
            'ph': bf(np.random.uniform(-np.pi, np.pi, (B, S, D)) * s),
            'cr': bf(n((B, S, D)) * 1.1 * t),
            'ci': bf(n((B, S, D)) * 1.1 * t),
            'Wa': bf(n((D, D)) * wg / s[:, None]), 'ba': bf(n(D) * 0.2),
            'Wp': bf(n((D, D)) * wg / s[:, None]), 'bp': bf(n(D) * 0.2),
            'gate_bias': bf(n(D) * 0.2),
            'w1r': bf(n((D, F)) * wu / t[:, None]), 'b1r': bf(n(F) * 0.2),
            'w1i': bf(n((D, F)) * wu / t[:, None]), 'b1i': bf(n(F) * 0.2)}


def reference(amp, ph, cr, ci, Wa, ba, Wp, bp, gate_bias, w1r, b1r, w1i, b1i):
    za = mxq(f64(amp), 2, 'e4m3') @ mxq(f64(Wa), 0, 'e4m3')
    zp = mxq(f64(ph), 2, 'e4m3') @ mxq(f64(Wp), 0, 'e4m3')
    gate = sigmoid(za + f64(ba) + zp + f64(bp) + f64(gate_bias))
    gr = f64(cr) * gate
    gi = f64(ci) * gate
    h_r = gelu((mxq(gr, 2, 'e4m3') @ mxq(f64(w1r), 0, 'e4m3')) + f64(b1r))
    h_i = gelu((mxq(gi, 2, 'e4m3') @ mxq(f64(w1i), 0, 'e4m3')) + f64(b1i))
    return h_r, h_i

@@ -1,0 +1,256 @@
+from contextlib import ExitStack
+
+import concourse.mybir as mybir
+from concourse.masks import make_identity
+
+F32 = mybir.dt.float32
+BF16 = mybir.dt.bfloat16
+U32 = mybir.dt.uint32
+U8 = mybir.dt.uint8
+FP8X4 = mybir.dt.float8_e4m3fn_x4
+ACT = mybir.ActivationFunctionType
+ALU = mybir.AluOpType
+AXIS = mybir.AxisListType
+
+P = 128
+PACK = 4
+TOKENS = 1024
+TOKEN_TILES = TOKENS // P
+D = 512
+F = 2048
+BANK = 512
+HALF = 512
+GROUP = 256
+STORE = 1024
+
+FLOPS = 2 * TOKENS * D * (2 * D + 2 * F)
+
+
+def tile_wavenetworklm_pa_kernel(
+    tc, amp, ph, cr, ci, Wa, ba, Wp, bp, gate_bias, w1r, b1r, w1i, b1i, out_0, out_1
+):
+    nc = tc.nc
+    with ExitStack() as stack:
+        keep = stack.enter_context(tc.tile_pool(name="keep", bufs=1))
+        stage = stack.enter_context(tc.tile_pool(name="stage", bufs=3))
+        results = stack.enter_context(tc.tile_pool(name="results", bufs=8))
+        banks = stack.enter_context(tc.psum_pool(name="banks", bufs=8))
+
+        ident_f32 = keep.tile([P, P], F32, name="ident_f32")
+        make_identity(nc, ident_f32[:])
+        ident_bf16 = keep.tile([P, P], BF16, name="ident_bf16")
+        make_identity(nc, ident_bf16[:])
+        bias_rows = keep.tile([P, P], BF16, name="bias_rows")
+        nc.vector.memset(bias_rows[:], 0.0)
+
+        def token_view(x):
+            return x.flatten_outer_dims().rearrange("(p a) c -> p (a c)", a=TOKEN_TILES)
+
+        def load_tokens(x, name, pieces):
+            x_sb = keep.tile([P, TOKEN_TILES * D], BF16, name=name)
+            return x_sb, [
+                (x_sb[:, cols], token_view(x)[:, cols])
+                for cols in [
+                    slice(i * TOKEN_TILES * D // pieces, (i + 1) * TOKEN_TILES * D // pieces)
+                    for i in range(pieces)
+                ]
+            ]
+
+        def start_load(piece):
+            nc.sync.dma_start(out=piece[0], in_=piece[1])
+
+        def load_gate_weight(w, name):
+            raw = keep.tile([P, PACK, D], BF16, name=name)
+            nc.sync.dma_start(
+                out=raw[:].rearrange("p (u e) n -> p u e n", e=2),
+                in_=w.rearrange("(u p e) n -> p u e n", u=2, e=2),
+            )
+            return raw
+
+        def load_up_weight(w, name):
+            raw = keep.tile([P, PACK, F], BF16, name=name)
+            for cols in (slice(0, F // 2), slice(F // 2, F)):
+                nc.sync.dma_start(
+                    out=raw[:, :, cols], in_=w.rearrange("(t p) n -> p t n", p=P)[:, :, cols]
+                )
+            return raw
+
+        def load_row_bias(b, name):
+            spread = keep.tile([P, F], BF16, name=name)
+            nc.sync.dma_start(out=spread[:], in_=b.partition_broadcast(P))
+            return spread
+
+        amp_sb, amp_pieces = load_tokens(amp, "amp_sb", 2)
+        ph_sb, ph_pieces = load_tokens(ph, "ph_sb", 2)
+        cr_sb, cr_pieces = load_tokens(cr, "cr_sb", 1)
+        ci_sb, ci_pieces = load_tokens(ci, "ci_sb", 1)
+
+        wa_raw = load_gate_weight(Wa, "wa_raw")
+        start_load(amp_pieces[0])
+        wp_raw = load_gate_weight(Wp, "wp_raw")
+        start_load(ph_pieces[0])
+        for j, vec in enumerate((ba, bp, gate_bias)):
+            nc.sync.dma_start(
+                out=bias_rows[PACK * j : PACK * (j + 1), :], in_=vec.rearrange("(m p) -> m p", p=P)
+            )
+        start_load(amp_pieces[1])
+        start_load(ph_pieces[1])
+        start_load(cr_pieces[0])
+        b1r_spread = load_row_bias(b1r, "b1r_spread")
+        w1r_raw = load_up_weight(w1r, "w1r_raw")
+        start_load(ci_pieces[0])
+        b1i_spread = load_row_bias(b1i, "b1i_spread")
+        w1i_raw = load_up_weight(w1i, "w1i_raw")
+
+        def quantise(codes, scales, grouped):
+            nc.vector.quantize_mx(out=codes.bitcast(FP8X4), scales=scales, in_=grouped)
+
+        def quantise_weight(raw, codes, scales, copies):
+            for c in range(raw.shape[2] // BANK):
+                cols = slice(c * BANK, (c + 1) * BANK)
+                grouped = stage.tile([P, BANK, PACK], BF16, name="w_grouped", align_bytes=64)
+                copies[c % len(copies)](
+                    out=grouped[:].rearrange("p (c i) t -> p c t i", i=4),
+                    in_=raw[:, :, cols].rearrange("p t (c i) -> p c t i", i=4),
+                )
+                quantise(codes[:, cols], scales[:, cols], grouped[:].rearrange("p c t -> p (c t)"))
+
+        def mx_tiles(name, width):
+            codes = keep.tile([P, width], U32, name=name + "_codes", align_bytes=64)
+            scales = keep.tile([P, width], U8, name=name + "_scales", align_bytes=64)
+            return codes, scales
+
+        wa_codes, wa_scales = mx_tiles("wa", D)
+        wp_codes, wp_scales = mx_tiles("wp", D)
+        quantise_weight(wa_raw, wa_codes, wa_scales, [nc.vector.tensor_copy])
+        quantise_weight(wp_raw, wp_codes, wp_scales, [nc.vector.tensor_copy])
+
+        bias_cols_ps = banks.tile([P, P], BF16, name="bias_cols_ps", tag="bank")
+        nc.tensor.transpose(out=bias_cols_ps[:], in_=bias_rows[:], identity=ident_bf16[:])
+        bias_cols = keep.tile([P, 3 * PACK], F32, name="bias_cols")
+        nc.vector.tensor_copy(out=bias_cols[:], in_=bias_cols_ps[:, 0 : 3 * PACK])
+        gate_shift = keep.tile([P, PACK], F32, name="gate_shift")
+        nc.vector.tensor_reduce(
+            out=gate_shift[:],
+            in_=bias_cols[:].rearrange("p (j m) -> p m j", m=PACK),
+            axis=AXIS.X,
+            op=ALU.add,
+        )
+
+        amp_codes, amp_scales = mx_tiles("amp", TOKENS)
+        ph_codes, ph_scales = mx_tiles("ph", TOKENS)
+        gate = keep.tile([P, PACK, TOKENS], F32, name="gate")
+
+        def quantise_tokens_k_last(x_sb, codes, scales, h):
+            x_words = x_sb[:].bitcast(F32)
+            grouped = stage.tile([P, HALF * PACK], BF16, name="x_grouped", align_bytes=64)
+            grouped_words = grouped[:].bitcast(F32).rearrange("p (w u) -> p w u", u=2)
+            for g in range(HALF // GROUP):
+                words_t = banks.tile([P, 2, GROUP], F32, name="words_t", tag="bank")
+                for j in range(GROUP // P):
+                    a = (h * HALF + g * GROUP) // P + j
+                    for u in range(2):
+                        first = a * (D // 2) + u * P
+                        nc.tensor.transpose(
+                            out=words_t[:, u, j * P : (j + 1) * P],
+                            in_=x_words[:, first : first + P],
+                            identity=ident_f32[:],
+                        )
+                nc.scalar.copy(
+                    out=grouped_words[:, g * GROUP : (g + 1) * GROUP, :],
+                    in_=words_t[:].rearrange("p u w -> p w u"),
+                )
+            cols = slice(h * HALF, (h + 1) * HALF)
+            quantise(codes[:, cols], scales[:, cols], grouped[:])
+
+        for h in range(TOKENS // HALF):
+            quantise_tokens_k_last(amp_sb, amp_codes, amp_scales, h)
+            quantise_tokens_k_last(ph_sb, ph_codes, ph_scales, h)
+            cols = slice(h * HALF, (h + 1) * HALF)
+            for m in range(PACK):
+                rows = slice(m * P, (m + 1) * P)
+                z = banks.tile([P, HALF], F32, name="z", tag="bank")
+                nc.tensor.matmul_mx(
+                    out=z[:],
+                    lhsT=wa_codes[:, rows].bitcast(FP8X4),
+                    lhsT_scale=wa_scales[:, rows],
+                    rhs=amp_codes[:, cols].bitcast(FP8X4),
+                    rhs_scale=amp_scales[:, cols],
+                    start=True,
+                    stop=False,
+                )
+                nc.tensor.matmul_mx(
+                    out=z[:],
+                    lhsT=wp_codes[:, rows].bitcast(FP8X4),
+                    lhsT_scale=wp_scales[:, rows],
+                    rhs=ph_codes[:, cols].bitcast(FP8X4),
+                    rhs_scale=ph_scales[:, cols],
+                    start=False,
+                    stop=True,
+                )
+                nc.scalar.activation(
+                    out=gate[:, m, cols], in_=z[:], func=ACT.Sigmoid, bias=gate_shift[:, m : m + 1]
+                )
+
+        def quantise_gated(x_sb, codes, scales):
+            for g in range(TOKENS // GROUP):
+                x_t = banks.tile([P, PACK, GROUP], BF16, name="x_t", tag="bank")
+                for j in range(GROUP // P):
+                    a = g * GROUP // P + j
+                    for t in range(PACK):
+                        first = a * D + t * P
+                        nc.tensor.transpose(
+                            out=x_t[:, t, j * P : (j + 1) * P],
+                            in_=x_sb[:, first : first + P],
+                            identity=ident_bf16[:],
+                        )
+                cols = slice(g * GROUP, (g + 1) * GROUP)
+                gated = stage.tile([P, GROUP, PACK], BF16, name="gated", align_bytes=64)
+                nc.vector.tensor_tensor(
+                    out=gated[:],
+                    in0=x_t[:].rearrange("p t w -> p w t"),
+                    in1=gate[:, :, cols].rearrange("p t w -> p w t"),
+                    op=ALU.mult,
+                )
+                quantise(codes[:, cols], scales[:, cols], gated[:].rearrange("p w t -> p (w t)"))
+
+        gr_codes, gr_scales = mx_tiles("gr", TOKENS)
+        gi_codes, gi_scales = mx_tiles("gi", TOKENS)
+        w1r_codes, w1r_scales = mx_tiles("w1r", F)
+        w1i_codes, w1i_scales = mx_tiles("w1i", F)
+        quantise_gated(cr_sb, gr_codes, gr_scales)
+        quantise_weight(w1r_raw, w1r_codes, w1r_scales, [nc.vector.tensor_copy, nc.scalar.copy])
+        quantise_gated(ci_sb, gi_codes, gi_scales)
+        quantise_weight(w1i_raw, w1i_codes, w1i_scales, [nc.vector.tensor_copy, nc.scalar.copy])
+
+        def up_project(x_codes, x_scales, w_codes, w_scales, bias_spread, out):
+            out_view = out.flatten_outer_dims().rearrange("(p a) f -> p a f", a=TOKEN_TILES)
+            for a in range(TOKEN_TILES):
+                rows = slice(a * P, (a + 1) * P)
+                for s in range(F // STORE):
+                    result = results.tile([P, STORE], F32, name="result")
+                    for c in range(STORE // BANK):
+                        cols = slice(s * STORE + c * BANK, s * STORE + (c + 1) * BANK)
+                        acc = banks.tile([P, BANK], F32, name="acc", tag="bank")
+                        nc.tensor.matmul_mx(
+                            out=acc[:],
+                            lhsT=x_codes[:, rows].bitcast(FP8X4),
+                            lhsT_scale=x_scales[:, rows],
+                            rhs=w_codes[:, cols].bitcast(FP8X4),
+                            rhs_scale=w_scales[:, cols],
+                            start=True,
+                            stop=True,
+                        )
+                        nc.vector.tensor_tensor(
+                            out=result[:, c * BANK : (c + 1) * BANK],
+                            in0=acc[:],
+                            in1=bias_spread[:, cols],
+                            op=ALU.add,
+                        )
+                    nc.scalar.activation(out=result[:], in_=result[:], func=ACT.Gelu)
+                    nc.sync.dma_start(
+                        out=out_view[:, a, s * STORE : (s + 1) * STORE], in_=result[:]
+                    )
+
+        up_project(gr_codes, gr_scales, w1r_codes, w1r_scales, b1r_spread, out_0)
+        up_project(gi_codes, gi_scales, w1i_codes, w1i_scales, b1i_spread, out_1)

@@ -22,6 +22,7 @@ BANK = 512
 HALF = 512
 GROUP = 256
 STORE = 1024
+PIECE = 256
 
 FLOPS = 2 * TOKENS * D * (2 * D + 2 * F)
 
@@ -40,110 +41,114 @@ def tile_wavenetworklm_pa_kernel(
         make_identity(nc, ident_f32[:])
         ident_bf16 = keep.tile([P, P], BF16, name="ident_bf16")
         make_identity(nc, ident_bf16[:])
-        bias_rows = keep.tile([P, P], BF16, name="bias_rows")
-        nc.vector.memset(bias_rows[:], 0.0)
+        gate_bias_rows = keep.tile([P, P], BF16, name="gate_bias_rows")
+        nc.vector.memset(gate_bias_rows[:], 0.0)
+        up_bias_rows = keep.tile([P, F], BF16, name="up_bias_rows")
+        nc.gpsimd.memset(up_bias_rows[:], 0.0)
 
-        def token_view(x):
-            return x.flatten_outer_dims().rearrange("(p a) c -> p (a c)", a=TOKEN_TILES)
+        nc.scalar.dma_start(out=up_bias_rows[0:1, :], in_=b1r.rearrange("(o f) -> o f", o=1))
+        nc.scalar.dma_start(out=up_bias_rows[1:2, :], in_=b1i.rearrange("(o f) -> o f", o=1))
+        for j, vec in enumerate((ba, bp, gate_bias)):
+            nc.scalar.dma_start(
+                out=gate_bias_rows[PACK * j : PACK * (j + 1), :],
+                in_=vec.rearrange("(m p) -> m p", p=P),
+            )
 
-        def load_tokens(x, name, pieces):
-            x_sb = keep.tile([P, TOKEN_TILES * D], BF16, name=name)
-            return x_sb, [
-                (x_sb[:, cols], token_view(x)[:, cols])
-                for cols in [
-                    slice(i * TOKEN_TILES * D // pieces, (i + 1) * TOKEN_TILES * D // pieces)
-                    for i in range(pieces)
-                ]
-            ]
+        def load_token_half(x_sb, x, h):
+            cols = slice(h * HALF // P * D, (h + 1) * HALF // P * D)
+            x_view = x.flatten_outer_dims().rearrange("(p a) c -> p (a c)", a=TOKEN_TILES)
+            nc.sync.dma_start(out=x_sb[:, cols], in_=x_view[:, cols])
 
-        def start_load(piece):
-            nc.sync.dma_start(out=piece[0], in_=piece[1])
-
-        def load_gate_weight(w, name):
-            raw = keep.tile([P, PACK, D], BF16, name=name)
+        def load_gate_weight(raw, w):
             nc.sync.dma_start(
                 out=raw[:].rearrange("p (u e) n -> p u e n", e=2),
                 in_=w.rearrange("(u p e) n -> p u e n", u=2, e=2),
             )
-            return raw
 
-        def load_up_weight(w, name):
-            raw = keep.tile([P, PACK, F], BF16, name=name)
-            for cols in (slice(0, F // 2), slice(F // 2, F)):
-                nc.sync.dma_start(
-                    out=raw[:, :, cols], in_=w.rearrange("(t p) n -> p t n", p=P)[:, :, cols]
-                )
-            return raw
-
-        def load_row_bias(b, name):
-            spread = keep.tile([P, F], BF16, name=name)
-            nc.sync.dma_start(out=spread[:], in_=b.partition_broadcast(P))
-            return spread
-
-        amp_sb, amp_pieces = load_tokens(amp, "amp_sb", 2)
-        ph_sb, ph_pieces = load_tokens(ph, "ph_sb", 2)
-        cr_sb, cr_pieces = load_tokens(cr, "cr_sb", 1)
-        ci_sb, ci_pieces = load_tokens(ci, "ci_sb", 1)
-
-        wa_raw = load_gate_weight(Wa, "wa_raw")
-        start_load(amp_pieces[0])
-        wp_raw = load_gate_weight(Wp, "wp_raw")
-        start_load(ph_pieces[0])
-        for j, vec in enumerate((ba, bp, gate_bias)):
+        def load_up_weight_half(raw, w, s):
+            cols = slice(s * STORE, (s + 1) * STORE)
             nc.sync.dma_start(
-                out=bias_rows[PACK * j : PACK * (j + 1), :], in_=vec.rearrange("(m p) -> m p", p=P)
+                out=raw[:, :, cols], in_=w.rearrange("(t p) n -> p t n", p=P)[:, :, cols]
             )
-        start_load(amp_pieces[1])
-        start_load(ph_pieces[1])
-        start_load(cr_pieces[0])
-        b1r_spread = load_row_bias(b1r, "b1r_spread")
-        w1r_raw = load_up_weight(w1r, "w1r_raw")
-        start_load(ci_pieces[0])
-        b1i_spread = load_row_bias(b1i, "b1i_spread")
-        w1i_raw = load_up_weight(w1i, "w1i_raw")
 
-        def quantise(codes, scales, grouped):
-            nc.vector.quantize_mx(out=codes.bitcast(FP8X4), scales=scales, in_=grouped)
+        amp_sb = keep.tile([P, TOKEN_TILES * D], BF16, name="amp_sb")
+        ph_sb = keep.tile([P, TOKEN_TILES * D], BF16, name="ph_sb")
+        cr_sb = keep.tile([P, TOKEN_TILES * D], BF16, name="cr_sb")
+        ci_sb = keep.tile([P, TOKEN_TILES * D], BF16, name="ci_sb")
+        wa_raw = keep.tile([P, PACK, D], BF16, name="wa_raw")
+        wp_raw = keep.tile([P, PACK, D], BF16, name="wp_raw")
+        w1r_raw = keep.tile([P, PACK, F], BF16, name="w1r_raw")
+        w1i_raw = keep.tile([P, PACK, F], BF16, name="w1i_raw")
 
-        def quantise_weight(raw, codes, scales, copies):
-            for c in range(raw.shape[2] // BANK):
-                cols = slice(c * BANK, (c + 1) * BANK)
-                grouped = stage.tile([P, BANK, PACK], BF16, name="w_grouped", align_bytes=64)
-                copies[c % len(copies)](
-                    out=grouped[:].rearrange("p (c i) t -> p c t i", i=4),
-                    in_=raw[:, :, cols].rearrange("p t (c i) -> p c t i", i=4),
-                )
-                quantise(codes[:, cols], scales[:, cols], grouped[:].rearrange("p c t -> p (c t)"))
+        load_gate_weight(wa_raw, Wa)
+        load_gate_weight(wp_raw, Wp)
+        load_token_half(amp_sb, amp, 0)
+        load_token_half(ph_sb, ph, 0)
+        load_token_half(amp_sb, amp, 1)
+        load_token_half(ph_sb, ph, 1)
+        load_up_weight_half(w1r_raw, w1r, 0)
+        load_token_half(cr_sb, cr, 0)
+        load_token_half(cr_sb, cr, 1)
+        load_up_weight_half(w1r_raw, w1r, 1)
+        load_token_half(ci_sb, ci, 0)
+        load_token_half(ci_sb, ci, 1)
+        load_up_weight_half(w1i_raw, w1i, 0)
+        load_up_weight_half(w1i_raw, w1i, 1)
 
         def mx_tiles(name, width):
             codes = keep.tile([P, width], U32, name=name + "_codes", align_bytes=64)
             scales = keep.tile([P, width], U8, name=name + "_scales", align_bytes=64)
             return codes, scales
 
-        wa_codes, wa_scales = mx_tiles("wa", D)
-        wp_codes, wp_scales = mx_tiles("wp", D)
-        quantise_weight(wa_raw, wa_codes, wa_scales, [nc.vector.tensor_copy])
-        quantise_weight(wp_raw, wp_codes, wp_scales, [nc.vector.tensor_copy])
+        def quantise(mx, cols, grouped):
+            codes, scales = mx
+            nc.vector.quantize_mx(
+                out=codes[:, cols].bitcast(FP8X4), scales=scales[:, cols], in_=grouped
+            )
 
-        bias_cols_ps = banks.tile([P, P], BF16, name="bias_cols_ps", tag="bank")
-        nc.tensor.transpose(out=bias_cols_ps[:], in_=bias_rows[:], identity=ident_bf16[:])
-        bias_cols = keep.tile([P, 3 * PACK], F32, name="bias_cols")
-        nc.vector.tensor_copy(out=bias_cols[:], in_=bias_cols_ps[:, 0 : 3 * PACK])
-        gate_shift = keep.tile([P, PACK], F32, name="gate_shift")
-        nc.vector.tensor_reduce(
-            out=gate_shift[:],
-            in_=bias_cols[:].rearrange("p (j m) -> p m j", m=PACK),
-            axis=AXIS.X,
-            op=ALU.add,
-        )
+        def multiply_mx(out, stationary, rows, moving, cols, start, stop):
+            nc.tensor.matmul_mx(
+                out=out,
+                lhsT=stationary[0][:, rows].bitcast(FP8X4),
+                lhsT_scale=stationary[1][:, rows],
+                rhs=moving[0][:, cols].bitcast(FP8X4),
+                rhs_scale=moving[1][:, cols],
+                start=start,
+                stop=stop,
+            )
 
-        amp_codes, amp_scales = mx_tiles("amp", TOKENS)
-        ph_codes, ph_scales = mx_tiles("ph", TOKENS)
+        def regrouped_views(grouped, raw):
+            return (
+                grouped[:].rearrange("p (c i) t -> p c t i", i=4),
+                raw.rearrange("p t (c i) -> p c t i", i=4),
+            )
+
+        def regroup_on_vector(grouped, raw):
+            dst, src = regrouped_views(grouped, raw)
+            nc.vector.tensor_copy(out=dst, in_=src)
+
+        def regroup_on_gpsimd(grouped, raw):
+            dst, src = regrouped_views(grouped, raw)
+            nc.gpsimd.tensor_scalar(
+                out=dst, in0=src, scalar1=1.0, scalar2=0.0, op0=ALU.mult, op1=ALU.add
+            )
+
+        wa_mx = mx_tiles("wa", D)
+        wp_mx = mx_tiles("wp", D)
+        wa_grouped = stage.tile([P, D, PACK], BF16, name="wa_grouped", bufs=1, align_bytes=64)
+        wp_grouped = stage.tile([P, D, PACK], BF16, name="wp_grouped", bufs=1, align_bytes=64)
+        regroup_on_vector(wa_grouped, wa_raw[:])
+        regroup_on_vector(wp_grouped, wp_raw[:])
+        quantise(wa_mx, slice(0, D), wa_grouped[:].rearrange("p c t -> p (c t)"))
+        quantise(wp_mx, slice(0, D), wp_grouped[:].rearrange("p c t -> p (c t)"))
+
+        amp_mx = mx_tiles("amp", TOKENS)
+        ph_mx = mx_tiles("ph", TOKENS)
         gate = keep.tile([P, PACK, TOKENS], F32, name="gate")
 
-        def quantise_tokens_k_last(x_sb, codes, scales, h):
+        def quantise_token_half(x_sb, x_mx, h):
             x_words = x_sb[:].bitcast(F32)
-            grouped = stage.tile([P, HALF * PACK], BF16, name="x_grouped", align_bytes=64)
+            grouped = stage.tile([P, HALF * PACK], BF16, name="x_grouped", bufs=4, align_bytes=64)
             grouped_words = grouped[:].bitcast(F32).rearrange("p (w u) -> p w u", u=2)
             for g in range(HALF // GROUP):
                 words_t = banks.tile([P, 2, GROUP], F32, name="words_t", tag="bank")
@@ -160,97 +165,143 @@ def tile_wavenetworklm_pa_kernel(
                     out=grouped_words[:, g * GROUP : (g + 1) * GROUP, :],
                     in_=words_t[:].rearrange("p u w -> p w u"),
                 )
-            cols = slice(h * HALF, (h + 1) * HALF)
-            quantise(codes[:, cols], scales[:, cols], grouped[:])
+            quantise(x_mx, slice(h * HALF, (h + 1) * HALF), grouped[:])
 
-        for h in range(TOKENS // HALF):
-            quantise_tokens_k_last(amp_sb, amp_codes, amp_scales, h)
-            quantise_tokens_k_last(ph_sb, ph_codes, ph_scales, h)
+        def gate_half(h):
             cols = slice(h * HALF, (h + 1) * HALF)
             for m in range(PACK):
                 rows = slice(m * P, (m + 1) * P)
                 z = banks.tile([P, HALF], F32, name="z", tag="bank")
-                nc.tensor.matmul_mx(
-                    out=z[:],
-                    lhsT=wa_codes[:, rows].bitcast(FP8X4),
-                    lhsT_scale=wa_scales[:, rows],
-                    rhs=amp_codes[:, cols].bitcast(FP8X4),
-                    rhs_scale=amp_scales[:, cols],
-                    start=True,
-                    stop=False,
-                )
-                nc.tensor.matmul_mx(
-                    out=z[:],
-                    lhsT=wp_codes[:, rows].bitcast(FP8X4),
-                    lhsT_scale=wp_scales[:, rows],
-                    rhs=ph_codes[:, cols].bitcast(FP8X4),
-                    rhs_scale=ph_scales[:, cols],
-                    start=False,
-                    stop=True,
-                )
+                multiply_mx(z[:], wa_mx, rows, amp_mx, cols, True, False)
+                multiply_mx(z[:], wp_mx, rows, ph_mx, cols, False, True)
                 nc.scalar.activation(
                     out=gate[:, m, cols], in_=z[:], func=ACT.Sigmoid, bias=gate_shift[:, m : m + 1]
                 )
 
-        def quantise_gated(x_sb, codes, scales):
-            for g in range(TOKENS // GROUP):
-                x_t = banks.tile([P, PACK, GROUP], BF16, name="x_t", tag="bank")
-                for j in range(GROUP // P):
-                    a = g * GROUP // P + j
-                    for t in range(PACK):
-                        first = a * D + t * P
-                        nc.tensor.transpose(
-                            out=x_t[:, t, j * P : (j + 1) * P],
-                            in_=x_sb[:, first : first + P],
-                            identity=ident_bf16[:],
-                        )
-                cols = slice(g * GROUP, (g + 1) * GROUP)
-                gated = stage.tile([P, GROUP, PACK], BF16, name="gated", align_bytes=64)
-                nc.vector.tensor_tensor(
-                    out=gated[:],
-                    in0=x_t[:].rearrange("p t w -> p w t"),
-                    in1=gate[:, :, cols].rearrange("p t w -> p w t"),
-                    op=ALU.mult,
-                )
-                quantise(codes[:, cols], scales[:, cols], gated[:].rearrange("p w t -> p (w t)"))
+        for h in range(TOKENS // HALF):
+            quantise_token_half(amp_sb, amp_mx, h)
+            quantise_token_half(ph_sb, ph_mx, h)
+        bias_cols_ps = banks.tile([P, P], BF16, name="bias_cols_ps", tag="bank")
+        nc.tensor.transpose(out=bias_cols_ps[:], in_=gate_bias_rows[:], identity=ident_bf16[:])
+        bias_cols = keep.tile([P, 3 * PACK], F32, name="bias_cols")
+        nc.vector.tensor_copy(out=bias_cols[:], in_=bias_cols_ps[:, 0 : 3 * PACK])
+        gate_shift = keep.tile([P, PACK], F32, name="gate_shift")
+        nc.vector.tensor_reduce(
+            out=gate_shift[:],
+            in_=bias_cols[:].rearrange("p (j m) -> p m j", m=PACK),
+            axis=AXIS.X,
+            op=ALU.add,
+        )
 
-        gr_codes, gr_scales = mx_tiles("gr", TOKENS)
-        gi_codes, gi_scales = mx_tiles("gi", TOKENS)
-        w1r_codes, w1r_scales = mx_tiles("w1r", F)
-        w1i_codes, w1i_scales = mx_tiles("w1i", F)
-        quantise_gated(cr_sb, gr_codes, gr_scales)
-        quantise_weight(w1r_raw, w1r_codes, w1r_scales, [nc.vector.tensor_copy, nc.scalar.copy])
-        quantise_gated(ci_sb, gi_codes, gi_scales)
-        quantise_weight(w1i_raw, w1i_codes, w1i_scales, [nc.vector.tensor_copy, nc.scalar.copy])
+        for h in range(TOKENS // HALF):
+            gate_half(h)
 
-        def up_project(x_codes, x_scales, w_codes, w_scales, bias_spread, out):
-            out_view = out.flatten_outer_dims().rearrange("(p a) f -> p a f", a=TOKEN_TILES)
-            for a in range(TOKEN_TILES):
-                rows = slice(a * P, (a + 1) * P)
-                for s in range(F // STORE):
-                    result = results.tile([P, STORE], F32, name="result")
-                    for c in range(STORE // BANK):
-                        cols = slice(s * STORE + c * BANK, s * STORE + (c + 1) * BANK)
-                        acc = banks.tile([P, BANK], F32, name="acc", tag="bank")
-                        nc.tensor.matmul_mx(
-                            out=acc[:],
-                            lhsT=x_codes[:, rows].bitcast(FP8X4),
-                            lhsT_scale=x_scales[:, rows],
-                            rhs=w_codes[:, cols].bitcast(FP8X4),
-                            rhs_scale=w_scales[:, cols],
-                            start=True,
-                            stop=True,
-                        )
-                        nc.vector.tensor_tensor(
-                            out=result[:, c * BANK : (c + 1) * BANK],
-                            in0=acc[:],
-                            in1=bias_spread[:, cols],
-                            op=ALU.add,
-                        )
-                    nc.scalar.activation(out=result[:], in_=result[:], func=ACT.Gelu)
-                    nc.sync.dma_start(
-                        out=out_view[:, a, s * STORE : (s + 1) * STORE], in_=result[:]
+        real = {
+            "x": cr_sb,
+            "x_mx": mx_tiles("gr", TOKENS),
+            "w_raw": w1r_raw,
+            "w_mx": mx_tiles("w1r", F),
+            "bias_row": 0,
+            "bias": keep.tile([P, F], BF16, name="b1r_spread"),
+            "out": out_0.flatten_outer_dims().rearrange("(p a) f -> p a f", a=TOKEN_TILES),
+        }
+        imag = {
+            "x": ci_sb,
+            "x_mx": mx_tiles("gi", TOKENS),
+            "w_raw": w1i_raw,
+            "w_mx": mx_tiles("w1i", F),
+            "bias_row": 1,
+            "bias": keep.tile([P, F], BF16, name="b1i_spread"),
+            "out": out_1.flatten_outer_dims().rearrange("(p a) f -> p a f", a=TOKEN_TILES),
+        }
+
+        def multiply_by_gate(stream, g):
+            x_t = banks.tile([P, PACK, GROUP], BF16, name="x_t", tag="bank")
+            for j in range(GROUP // P):
+                a = g * GROUP // P + j
+                for t in range(PACK):
+                    first = a * D + t * P
+                    nc.tensor.transpose(
+                        out=x_t[:, t, j * P : (j + 1) * P],
+                        in_=stream["x"][:, first : first + P],
+                        identity=ident_bf16[:],
                     )
+            gated = stage.tile([P, GROUP, PACK], BF16, name="gated", align_bytes=64)
+            nc.vector.tensor_tensor(
+                out=gated[:],
+                in0=x_t[:].rearrange("p t w -> p w t"),
+                in1=gate[:, :, g * GROUP : (g + 1) * GROUP].rearrange("p t w -> p w t"),
+                op=ALU.mult,
+            )
+            return gated
 
-        up_project(gr_codes, gr_scales, w1r_codes, w1r_scales, b1r_spread, out_0)
-        up_project(gi_codes, gi_scales, w1i_codes, w1i_scales, b1i_spread, out_1)
+        def quantise_gated(stream, g, gated):
+            cols = slice(g * GROUP, (g + 1) * GROUP)
+            quantise(stream["x_mx"], cols, gated[:].rearrange("p w t -> p (w t)"))
+
+        def regroup_columns(stream, q, regroup):
+            grouped = stage.tile([P, PIECE, PACK], BF16, name="w_grouped", bufs=4, align_bytes=64)
+            regroup(grouped, stream["w_raw"][:, :, q * PIECE : (q + 1) * PIECE])
+            return grouped
+
+        def quantise_columns(stream, q, grouped):
+            cols = slice(q * PIECE, (q + 1) * PIECE)
+            quantise(stream["w_mx"], cols, grouped[:].rearrange("p c t -> p (c t)"))
+            j = stream["bias_row"]
+            spread_ps = banks.tile([P, PIECE], F32, name="spread_ps", tag="bank")
+            nc.tensor.matmul(
+                out=spread_ps[:],
+                lhsT=ident_bf16[:, j : j + 1].to_broadcast([P, P]),
+                rhs=up_bias_rows[:, cols],
+                start=True,
+                stop=True,
+            )
+            nc.scalar.copy(out=stream["bias"][:, cols], in_=spread_ps[:])
+
+        def up_project_tile(stream, s, a):
+            rows = slice(a * P, (a + 1) * P)
+            result = results.tile([P, STORE], F32, name="result")
+            for c in range(STORE // BANK):
+                cols = slice(s * STORE + c * BANK, s * STORE + (c + 1) * BANK)
+                acc = banks.tile([P, BANK], F32, name="acc", tag="bank")
+                multiply_mx(acc[:], stream["x_mx"], rows, stream["w_mx"], cols, True, True)
+                nc.vector.tensor_tensor(
+                    out=result[:, c * BANK : (c + 1) * BANK],
+                    in0=acc[:],
+                    in1=stream["bias"][:, cols],
+                    op=ALU.add,
+                )
+            nc.scalar.activation(out=result[:], in_=result[:], func=ACT.Gelu)
+            nc.sync.dma_start(out=stream["out"][:, a, s * STORE : (s + 1) * STORE], in_=result[:])
+
+        def up_project_half(stream, s, next_groups, next_columns):
+            gated = None
+            for a in range(TOKEN_TILES):
+                turn = a // 2
+                if a % 2 == 0 and turn < len(next_groups):
+                    gated = multiply_by_gate(next_groups[turn][0], next_groups[turn][1])
+                if a % 2 == 1 and turn < len(next_groups):
+                    quantise_gated(next_groups[turn][0], next_groups[turn][1], gated)
+                if a % 2 == 1 and turn < len(next_columns):
+                    piece_stream, q = next_columns[turn]
+                    quantise_columns(
+                        piece_stream, q, regroup_columns(piece_stream, q, regroup_on_gpsimd)
+                    )
+                up_project_tile(stream, s, a)
+
+        pieces = STORE // PIECE
+        groups = TOKENS // GROUP
+
+        first_pieces = [regroup_columns(real, q, regroup_on_vector) for q in range(pieces)]
+        for q in range(pieces):
+            quantise_columns(real, q, first_pieces[q])
+        quantise_gated(real, 0, multiply_by_gate(real, 0))
+
+        up_project_half(
+            real, 0, [(real, g) for g in range(1, groups)], [(real, pieces + q) for q in range(pieces)]
+        )
+        up_project_half(
+            real, 1, [(imag, g) for g in range(groups)], [(imag, q) for q in range(pieces)]
+        )
+        up_project_half(imag, 0, [], [(imag, pieces + q) for q in range(pieces)])
+        up_project_half(imag, 1, [], [])

@@ -23,6 +23,10 @@ HALF = 512
 GROUP = 256
 STORE = 1024
 PIECE = 256
+GATE_PIECES = D // PIECE
+HALF_PIECES = STORE // PIECE
+GROUPS = TOKENS // GROUP
+RESULT_BUFS = 8
 
 FLOPS = 2 * TOKENS * D * (2 * D + 2 * F)
 
@@ -33,72 +37,95 @@ def tile_wavenetworklm_pa_kernel(
     nc = tc.nc
     with ExitStack() as stack:
         keep = stack.enter_context(tc.tile_pool(name="keep", bufs=1))
-        stage = stack.enter_context(tc.tile_pool(name="stage", bufs=3))
-        results = stack.enter_context(tc.tile_pool(name="results", bufs=8))
+        stage = stack.enter_context(tc.tile_pool(name="stage", bufs=2))
+        results = stack.enter_context(tc.tile_pool(name="results", bufs=RESULT_BUFS))
         banks = stack.enter_context(tc.psum_pool(name="banks", bufs=8))
-
-        ident_f32 = keep.tile([P, P], F32, name="ident_f32")
-        make_identity(nc, ident_f32[:])
-        ident_bf16 = keep.tile([P, P], BF16, name="ident_bf16")
-        make_identity(nc, ident_bf16[:])
-        gate_bias_rows = keep.tile([P, P], BF16, name="gate_bias_rows")
-        nc.vector.memset(gate_bias_rows[:], 0.0)
-        up_bias_rows = keep.tile([P, F], BF16, name="up_bias_rows")
-        nc.gpsimd.memset(up_bias_rows[:], 0.0)
-
-        nc.scalar.dma_start(out=up_bias_rows[0:1, :], in_=b1r.rearrange("(o f) -> o f", o=1))
-        nc.scalar.dma_start(out=up_bias_rows[1:2, :], in_=b1i.rearrange("(o f) -> o f", o=1))
-        for j, vec in enumerate((ba, bp, gate_bias)):
-            nc.scalar.dma_start(
-                out=gate_bias_rows[PACK * j : PACK * (j + 1), :],
-                in_=vec.rearrange("(m p) -> m p", p=P),
-            )
-
-        def load_token_half(x_sb, x, h):
-            cols = slice(h * HALF // P * D, (h + 1) * HALF // P * D)
-            x_view = x.flatten_outer_dims().rearrange("(p a) c -> p (a c)", a=TOKEN_TILES)
-            nc.sync.dma_start(out=x_sb[:, cols], in_=x_view[:, cols])
-
-        def load_gate_weight(raw, w):
-            nc.sync.dma_start(
-                out=raw[:].rearrange("p (u e) n -> p u e n", e=2),
-                in_=w.rearrange("(u p e) n -> p u e n", u=2, e=2),
-            )
-
-        def load_up_weight_half(raw, w, s):
-            cols = slice(s * STORE, (s + 1) * STORE)
-            nc.sync.dma_start(
-                out=raw[:, :, cols], in_=w.rearrange("(t p) n -> p t n", p=P)[:, :, cols]
-            )
-
-        amp_sb = keep.tile([P, TOKEN_TILES * D], BF16, name="amp_sb")
-        ph_sb = keep.tile([P, TOKEN_TILES * D], BF16, name="ph_sb")
-        cr_sb = keep.tile([P, TOKEN_TILES * D], BF16, name="cr_sb")
-        ci_sb = keep.tile([P, TOKEN_TILES * D], BF16, name="ci_sb")
-        wa_raw = keep.tile([P, PACK, D], BF16, name="wa_raw")
-        wp_raw = keep.tile([P, PACK, D], BF16, name="wp_raw")
-        w1r_raw = keep.tile([P, PACK, F], BF16, name="w1r_raw")
-        w1i_raw = keep.tile([P, PACK, F], BF16, name="w1i_raw")
-
-        load_gate_weight(wa_raw, Wa)
-        load_gate_weight(wp_raw, Wp)
-        load_token_half(amp_sb, amp, 0)
-        load_token_half(ph_sb, ph, 0)
-        load_token_half(amp_sb, amp, 1)
-        load_token_half(ph_sb, ph, 1)
-        load_up_weight_half(w1r_raw, w1r, 0)
-        load_token_half(cr_sb, cr, 0)
-        load_token_half(cr_sb, cr, 1)
-        load_up_weight_half(w1r_raw, w1r, 1)
-        load_token_half(ci_sb, ci, 0)
-        load_token_half(ci_sb, ci, 1)
-        load_up_weight_half(w1i_raw, w1i, 0)
-        load_up_weight_half(w1i_raw, w1i, 1)
+        stack.enter_context(tc.manual_schedule())
 
         def mx_tiles(name, width):
             codes = keep.tile([P, width], U32, name=name + "_codes", align_bytes=64)
             scales = keep.tile([P, width], U8, name=name + "_scales", align_bytes=64)
             return codes, scales
+
+        ident_f32 = keep.tile([P, P], F32, name="ident_f32")
+        ident_bf16 = keep.tile([P, P], BF16, name="ident_bf16")
+        gate_bias_rows = keep.tile([P, P], BF16, name="gate_bias_rows")
+        up_bias_rows = keep.tile([P, F], BF16, name="up_bias_rows")
+        warm = keep.tile([P, 1], F32, name="warm")
+        gate_shift = keep.tile([P, PACK], F32, name="gate_shift")
+        gate = keep.tile([P, PACK, TOKENS], F32, name="gate")
+
+        amplitude = {
+            "x": keep.tile([P, TOKEN_TILES * D], BF16, name="amp_sb"),
+            "x_dram": amp,
+            "x_mx": mx_tiles("amp", TOKENS),
+            "w_raw": keep.tile([P, PACK, D], BF16, name="wa_raw"),
+            "w_dram": Wa,
+            "w_mx": mx_tiles("wa", D),
+        }
+        phase = {
+            "x": keep.tile([P, TOKEN_TILES * D], BF16, name="ph_sb"),
+            "x_dram": ph,
+            "x_mx": mx_tiles("ph", TOKENS),
+            "w_raw": keep.tile([P, PACK, D], BF16, name="wp_raw"),
+            "w_dram": Wp,
+            "w_mx": mx_tiles("wp", D),
+        }
+        real = {
+            "x": keep.tile([P, TOKEN_TILES * D], BF16, name="cr_sb"),
+            "x_dram": cr,
+            "x_mx": mx_tiles("gr", TOKENS),
+            "w_raw": keep.tile([P, PACK, F], BF16, name="w1r_raw"),
+            "w_dram": w1r,
+            "w_mx": mx_tiles("w1r", F),
+            "bias_dram": b1r,
+            "bias_row": 0,
+            "bias": keep.tile([P, F], BF16, name="b1r_spread"),
+            "out": out_0.flatten_outer_dims().rearrange("(p a) f -> p a f", a=TOKEN_TILES),
+        }
+        imag = {
+            "x": keep.tile([P, TOKEN_TILES * D], BF16, name="ci_sb"),
+            "x_dram": ci,
+            "x_mx": mx_tiles("gi", TOKENS),
+            "w_raw": keep.tile([P, PACK, F], BF16, name="w1i_raw"),
+            "w_dram": w1i,
+            "w_mx": mx_tiles("w1i", F),
+            "bias_dram": b1i,
+            "bias_row": 1,
+            "bias": keep.tile([P, F], BF16, name="b1i_spread"),
+            "out": out_1.flatten_outer_dims().rearrange("(p a) f -> p a f", a=TOKEN_TILES),
+        }
+
+        def load_token_half(stream, h):
+            cols = slice(h * HALF // P * D, (h + 1) * HALF // P * D)
+            x_view = stream["x_dram"].flatten_outer_dims().rearrange("(p a) c -> p (a c)", a=TOKEN_TILES)
+            nc.sync.dma_start(out=stream["x"][:, cols], in_=x_view[:, cols])
+
+        def load_gate_weight(stream):
+            nc.sync.dma_start(
+                out=stream["w_raw"][:].rearrange("p (u e) n -> p u e n", e=2),
+                in_=stream["w_dram"].rearrange("(u p e) n -> p u e n", u=2, e=2),
+            )
+
+        def load_up_weight_half(stream, s):
+            cols = slice(s * STORE, (s + 1) * STORE)
+            nc.sync.dma_start(
+                out=stream["w_raw"][:, :, cols],
+                in_=stream["w_dram"].rearrange("(t p) n -> p t n", p=P)[:, :, cols],
+            )
+
+        def load_gate_biases():
+            for j, vec in enumerate((ba, bp, gate_bias)):
+                nc.sync.dma_start(
+                    out=gate_bias_rows[PACK * j : PACK * (j + 1), :],
+                    in_=vec.rearrange("(m p) -> m p", p=P),
+                )
+
+        def load_up_bias(stream):
+            j = stream["bias_row"]
+            nc.sync.dma_start(
+                out=up_bias_rows[j : j + 1, :], in_=stream["bias_dram"].rearrange("(o f) -> o f", o=1)
+            )
 
         def quantise(mx, cols, grouped):
             codes, scales = mx
@@ -117,37 +144,36 @@ def tile_wavenetworklm_pa_kernel(
                 stop=stop,
             )
 
-        def regrouped_views(grouped, raw):
-            return (
-                grouped[:].rearrange("p (c i) t -> p c t i", i=4),
-                raw.rearrange("p t (c i) -> p c t i", i=4),
+        def regroup_columns(stream, q, on_gpsimd):
+            grouped = stage.tile([P, PIECE, PACK], BF16, name="w_grouped", bufs=4, align_bytes=64)
+            dst = grouped[:].rearrange("p (c i) t -> p c t i", i=4)
+            src = stream["w_raw"][:, :, q * PIECE : (q + 1) * PIECE].rearrange("p t (c i) -> p c t i", i=4)
+            if on_gpsimd:
+                nc.gpsimd.tensor_scalar(
+                    out=dst, in0=src, scalar1=1.0, scalar2=0.0, op0=ALU.mult, op1=ALU.add
+                )
+            else:
+                nc.vector.tensor_copy(out=dst, in_=src)
+            return grouped
+
+        def quantise_columns(stream, q, grouped):
+            quantise(stream["w_mx"], slice(q * PIECE, (q + 1) * PIECE), grouped[:].rearrange("p c t -> p (c t)"))
+
+        def spread_bias(stream, q):
+            cols = slice(q * PIECE, (q + 1) * PIECE)
+            j = stream["bias_row"]
+            spread_ps = banks.tile([P, PIECE], F32, name="spread_ps", tag="bank")
+            nc.tensor.matmul(
+                out=spread_ps[:],
+                lhsT=ident_bf16[:, j : j + 1].to_broadcast([P, P]),
+                rhs=up_bias_rows[:, cols],
+                start=True,
+                stop=True,
             )
+            nc.scalar.copy(out=stream["bias"][:, cols], in_=spread_ps[:])
 
-        def regroup_on_vector(grouped, raw):
-            dst, src = regrouped_views(grouped, raw)
-            nc.vector.tensor_copy(out=dst, in_=src)
-
-        def regroup_on_gpsimd(grouped, raw):
-            dst, src = regrouped_views(grouped, raw)
-            nc.gpsimd.tensor_scalar(
-                out=dst, in0=src, scalar1=1.0, scalar2=0.0, op0=ALU.mult, op1=ALU.add
-            )
-
-        wa_mx = mx_tiles("wa", D)
-        wp_mx = mx_tiles("wp", D)
-        wa_grouped = stage.tile([P, D, PACK], BF16, name="wa_grouped", bufs=1, align_bytes=64)
-        wp_grouped = stage.tile([P, D, PACK], BF16, name="wp_grouped", bufs=1, align_bytes=64)
-        regroup_on_vector(wa_grouped, wa_raw[:])
-        regroup_on_vector(wp_grouped, wp_raw[:])
-        quantise(wa_mx, slice(0, D), wa_grouped[:].rearrange("p c t -> p (c t)"))
-        quantise(wp_mx, slice(0, D), wp_grouped[:].rearrange("p c t -> p (c t)"))
-
-        amp_mx = mx_tiles("amp", TOKENS)
-        ph_mx = mx_tiles("ph", TOKENS)
-        gate = keep.tile([P, PACK, TOKENS], F32, name="gate")
-
-        def quantise_token_half(x_sb, x_mx, h):
-            x_words = x_sb[:].bitcast(F32)
+        def quantise_token_half(stream, h):
+            x_words = stream["x"][:].bitcast(F32)
             grouped = stage.tile([P, HALF * PACK], BF16, name="x_grouped", bufs=4, align_bytes=64)
             grouped_words = grouped[:].bitcast(F32).rearrange("p (w u) -> p w u", u=2)
             for g in range(HALF // GROUP):
@@ -165,57 +191,32 @@ def tile_wavenetworklm_pa_kernel(
                     out=grouped_words[:, g * GROUP : (g + 1) * GROUP, :],
                     in_=words_t[:].rearrange("p u w -> p w u"),
                 )
-            quantise(x_mx, slice(h * HALF, (h + 1) * HALF), grouped[:])
+            quantise(stream["x_mx"], slice(h * HALF, (h + 1) * HALF), grouped[:])
+
+        def sum_gate_biases():
+            bias_cols_ps = banks.tile([P, P], BF16, name="bias_cols_ps", tag="bank")
+            nc.tensor.transpose(out=bias_cols_ps[:], in_=gate_bias_rows[:], identity=ident_bf16[:])
+            bias_cols = keep.tile([P, 3 * PACK], F32, name="bias_cols")
+            nc.vector.tensor_copy(out=bias_cols[:], in_=bias_cols_ps[:, 0 : 3 * PACK])
+            nc.vector.tensor_reduce(
+                out=gate_shift[:],
+                in_=bias_cols[:].rearrange("p (j m) -> p m j", m=PACK),
+                axis=AXIS.X,
+                op=ALU.add,
+            )
 
         def gate_half(h):
             cols = slice(h * HALF, (h + 1) * HALF)
             for m in range(PACK):
                 rows = slice(m * P, (m + 1) * P)
                 z = banks.tile([P, HALF], F32, name="z", tag="bank")
-                multiply_mx(z[:], wa_mx, rows, amp_mx, cols, True, False)
-                multiply_mx(z[:], wp_mx, rows, ph_mx, cols, False, True)
+                multiply_mx(z[:], amplitude["w_mx"], rows, amplitude["x_mx"], cols, True, False)
+                multiply_mx(z[:], phase["w_mx"], rows, phase["x_mx"], cols, False, True)
                 nc.scalar.activation(
                     out=gate[:, m, cols], in_=z[:], func=ACT.Sigmoid, bias=gate_shift[:, m : m + 1]
                 )
 
-        for h in range(TOKENS // HALF):
-            quantise_token_half(amp_sb, amp_mx, h)
-            quantise_token_half(ph_sb, ph_mx, h)
-        bias_cols_ps = banks.tile([P, P], BF16, name="bias_cols_ps", tag="bank")
-        nc.tensor.transpose(out=bias_cols_ps[:], in_=gate_bias_rows[:], identity=ident_bf16[:])
-        bias_cols = keep.tile([P, 3 * PACK], F32, name="bias_cols")
-        nc.vector.tensor_copy(out=bias_cols[:], in_=bias_cols_ps[:, 0 : 3 * PACK])
-        gate_shift = keep.tile([P, PACK], F32, name="gate_shift")
-        nc.vector.tensor_reduce(
-            out=gate_shift[:],
-            in_=bias_cols[:].rearrange("p (j m) -> p m j", m=PACK),
-            axis=AXIS.X,
-            op=ALU.add,
-        )
-
-        for h in range(TOKENS // HALF):
-            gate_half(h)
-
-        real = {
-            "x": cr_sb,
-            "x_mx": mx_tiles("gr", TOKENS),
-            "w_raw": w1r_raw,
-            "w_mx": mx_tiles("w1r", F),
-            "bias_row": 0,
-            "bias": keep.tile([P, F], BF16, name="b1r_spread"),
-            "out": out_0.flatten_outer_dims().rearrange("(p a) f -> p a f", a=TOKEN_TILES),
-        }
-        imag = {
-            "x": ci_sb,
-            "x_mx": mx_tiles("gi", TOKENS),
-            "w_raw": w1i_raw,
-            "w_mx": mx_tiles("w1i", F),
-            "bias_row": 1,
-            "bias": keep.tile([P, F], BF16, name="b1i_spread"),
-            "out": out_1.flatten_outer_dims().rearrange("(p a) f -> p a f", a=TOKEN_TILES),
-        }
-
-        def multiply_by_gate(stream, g):
+        def transpose_group(stream, g):
             x_t = banks.tile([P, PACK, GROUP], BF16, name="x_t", tag="bank")
             for j in range(GROUP // P):
                 a = g * GROUP // P + j
@@ -226,37 +227,31 @@ def tile_wavenetworklm_pa_kernel(
                         in_=stream["x"][:, first : first + P],
                         identity=ident_bf16[:],
                     )
-            gated = stage.tile([P, GROUP, PACK], BF16, name="gated", align_bytes=64)
+            return x_t
+
+        def gate_view(g):
+            return gate[:, :, g * GROUP : (g + 1) * GROUP].rearrange("p t w -> p w t")
+
+        def multiply_by_gate_on_vector(stream, g):
+            x_t = transpose_group(stream, g)
+            gated = stage.tile([P, GROUP, PACK], BF16, name="gated_v", bufs=2, align_bytes=64)
             nc.vector.tensor_tensor(
-                out=gated[:],
-                in0=x_t[:].rearrange("p t w -> p w t"),
-                in1=gate[:, :, g * GROUP : (g + 1) * GROUP].rearrange("p t w -> p w t"),
-                op=ALU.mult,
+                out=gated[:], in0=x_t[:].rearrange("p t w -> p w t"), in1=gate_view(g), op=ALU.mult
+            )
+            return gated
+
+        def multiply_by_gate_on_gpsimd(stream, g):
+            x_t = transpose_group(stream, g)
+            x_t_sb = stage.tile([P, PACK, GROUP], BF16, name="x_t_sb", bufs=2)
+            nc.scalar.copy(out=x_t_sb[:], in_=x_t[:])
+            gated = stage.tile([P, GROUP, PACK], BF16, name="gated_g", bufs=4, align_bytes=64)
+            nc.gpsimd.tensor_tensor(
+                out=gated[:], in0=x_t_sb[:].rearrange("p t w -> p w t"), in1=gate_view(g), op=ALU.mult
             )
             return gated
 
         def quantise_gated(stream, g, gated):
-            cols = slice(g * GROUP, (g + 1) * GROUP)
-            quantise(stream["x_mx"], cols, gated[:].rearrange("p w t -> p (w t)"))
-
-        def regroup_columns(stream, q, regroup):
-            grouped = stage.tile([P, PIECE, PACK], BF16, name="w_grouped", bufs=4, align_bytes=64)
-            regroup(grouped, stream["w_raw"][:, :, q * PIECE : (q + 1) * PIECE])
-            return grouped
-
-        def quantise_columns(stream, q, grouped):
-            cols = slice(q * PIECE, (q + 1) * PIECE)
-            quantise(stream["w_mx"], cols, grouped[:].rearrange("p c t -> p (c t)"))
-            j = stream["bias_row"]
-            spread_ps = banks.tile([P, PIECE], F32, name="spread_ps", tag="bank")
-            nc.tensor.matmul(
-                out=spread_ps[:],
-                lhsT=ident_bf16[:, j : j + 1].to_broadcast([P, P]),
-                rhs=up_bias_rows[:, cols],
-                start=True,
-                stop=True,
-            )
-            nc.scalar.copy(out=stream["bias"][:, cols], in_=spread_ps[:])
+            quantise(stream["x_mx"], slice(g * GROUP, (g + 1) * GROUP), gated[:].rearrange("p w t -> p (w t)"))
 
         def up_project_tile(stream, s, a):
             rows = slice(a * P, (a + 1) * P)
@@ -274,34 +269,79 @@ def tile_wavenetworklm_pa_kernel(
             nc.scalar.activation(out=result[:], in_=result[:], func=ACT.Gelu)
             nc.sync.dma_start(out=stream["out"][:, a, s * STORE : (s + 1) * STORE], in_=result[:])
 
-        def up_project_half(stream, s, next_groups, next_columns):
-            gated = None
-            for a in range(TOKEN_TILES):
-                turn = a // 2
-                if a % 2 == 0 and turn < len(next_groups):
-                    gated = multiply_by_gate(next_groups[turn][0], next_groups[turn][1])
-                if a % 2 == 1 and turn < len(next_groups):
-                    quantise_gated(next_groups[turn][0], next_groups[turn][1], gated)
-                if a % 2 == 1 and turn < len(next_columns):
-                    piece_stream, q = next_columns[turn]
-                    quantise_columns(
-                        piece_stream, q, regroup_columns(piece_stream, q, regroup_on_gpsimd)
-                    )
-                up_project_tile(stream, s, a)
+        make_identity(nc, ident_f32[:])
+        make_identity(nc, ident_bf16[:])
+        nc.vector.memset(warm[:], 0.0)
+        nc.vector.memset(gate_bias_rows[:], 0.0)
+        nc.vector.memset(up_bias_rows[:], 0.0)
+        nc.scalar.activation(out=warm[:], in_=warm[:], func=ACT.Sigmoid)
+        load_gate_weight(amplitude)
+        load_gate_weight(phase)
+        load_gate_biases()
+        load_token_half(amplitude, 0)
+        load_token_half(phase, 0)
+        load_token_half(amplitude, 1)
+        load_token_half(phase, 1)
+        load_up_bias(real)
+        load_up_bias(imag)
+        load_up_weight_half(real, 0)
+        load_token_half(real, 0)
+        load_token_half(real, 1)
+        load_up_weight_half(real, 1)
+        load_token_half(imag, 0)
+        load_token_half(imag, 1)
+        load_up_weight_half(imag, 0)
+        load_up_weight_half(imag, 1)
+        regrouped = [regroup_columns(w, q, False) for w in (amplitude, phase) for q in range(GATE_PIECES)]
+        for i, w in enumerate((amplitude, phase)):
+            for q in range(GATE_PIECES):
+                quantise_columns(w, q, regrouped[i * GATE_PIECES + q])
+        quantise_token_half(amplitude, 0)
+        quantise_token_half(phase, 0)
+        quantise_token_half(amplitude, 1)
+        quantise_token_half(phase, 1)
+        sum_gate_biases()
+        gate_half(0)
+        gate_half(1)
+        regrouped = [regroup_columns(real, q, False) for q in range(HALF_PIECES)]
+        for q in range(HALF_PIECES):
+            quantise_columns(real, q, regrouped[q])
+        for q in range(HALF_PIECES):
+            spread_bias(real, q)
+        quantise_gated(real, 0, multiply_by_gate_on_vector(real, 0))
 
-        pieces = STORE // PIECE
-        groups = TOKENS // GROUP
+        regrouped = [regroup_columns(real, HALF_PIECES + q, True) for q in range(HALF_PIECES)]
+        gated_real = None
+        gated_imag = []
+        for a in range(TOKEN_TILES):
+            g = a // 2
+            if a % 2 == 0:
+                if g + 1 < GROUPS:
+                    gated_real = multiply_by_gate_on_vector(real, g + 1)
+                gated_imag.append(multiply_by_gate_on_gpsimd(imag, g))
+            else:
+                if g + 1 < GROUPS:
+                    quantise_gated(real, g + 1, gated_real)
+                quantise_columns(real, HALF_PIECES + g, regrouped[g])
+                spread_bias(real, HALF_PIECES + g)
+            up_project_tile(real, 0, a)
 
-        first_pieces = [regroup_columns(real, q, regroup_on_vector) for q in range(pieces)]
-        for q in range(pieces):
-            quantise_columns(real, q, first_pieces[q])
-        quantise_gated(real, 0, multiply_by_gate(real, 0))
+        regrouped = [regroup_columns(imag, q, True) for q in range(HALF_PIECES)]
+        for a in range(TOKEN_TILES):
+            g = a // 2
+            if a % 2 == 0:
+                quantise_gated(imag, g, gated_imag[g])
+            else:
+                quantise_columns(imag, g, regrouped[g])
+                spread_bias(imag, g)
+            up_project_tile(real, 1, a)
 
-        up_project_half(
-            real, 0, [(real, g) for g in range(1, groups)], [(real, pieces + q) for q in range(pieces)]
-        )
-        up_project_half(
-            real, 1, [(imag, g) for g in range(groups)], [(imag, q) for q in range(pieces)]
-        )
-        up_project_half(imag, 0, [], [(imag, pieces + q) for q in range(pieces)])
-        up_project_half(imag, 1, [], [])
+        regrouped = [regroup_columns(imag, HALF_PIECES + q, True) for q in range(HALF_PIECES)]
+        for a in range(TOKEN_TILES):
+            if a % 2 == 1:
+                quantise_columns(imag, HALF_PIECES + a // 2, regrouped[a // 2])
+                spread_bias(imag, HALF_PIECES + a // 2)
+            up_project_tile(imag, 0, a)
+
+        for a in range(TOKEN_TILES):
+            up_project_tile(imag, 1, a)

@@ -146,14 +146,21 @@ def tile_wavenetworklm_pa_kernel(
 
         def regroup_columns(stream, q, on_gpsimd):
             grouped = stage.tile([P, PIECE, PACK], BF16, name="w_grouped", bufs=4, align_bytes=64)
-            dst = grouped[:].rearrange("p (c i) t -> p c t i", i=4)
-            src = stream["w_raw"][:, :, q * PIECE : (q + 1) * PIECE].rearrange("p t (c i) -> p c t i", i=4)
+            raw = stream["w_raw"][:, :, q * PIECE : (q + 1) * PIECE]
             if on_gpsimd:
                 nc.gpsimd.tensor_scalar(
-                    out=dst, in0=src, scalar1=1.0, scalar2=0.0, op0=ALU.mult, op1=ALU.add
+                    out=grouped[:],
+                    in0=raw.rearrange("p t c -> p c t"),
+                    scalar1=1.0,
+                    scalar2=0.0,
+                    op0=ALU.mult,
+                    op1=ALU.add,
                 )
             else:
-                nc.vector.tensor_copy(out=dst, in_=src)
+                nc.vector.tensor_copy(
+                    out=grouped[:].rearrange("p (c i) t -> p c t i", i=4),
+                    in_=raw.rearrange("p t (c i) -> p c t i", i=4),
+                )
             return grouped
 
         def quantise_columns(stream, q, grouped):

@@ -146,21 +146,14 @@ def tile_wavenetworklm_pa_kernel(
 
         def regroup_columns(stream, q, on_gpsimd):
             grouped = stage.tile([P, PIECE, PACK], BF16, name="w_grouped", bufs=4, align_bytes=64)
-            raw = stream["w_raw"][:, :, q * PIECE : (q + 1) * PIECE]
+            dst = grouped[:].rearrange("p (c i) t -> p c t i", i=4)
+            src = stream["w_raw"][:, :, q * PIECE : (q + 1) * PIECE].rearrange("p t (c i) -> p c t i", i=4)
             if on_gpsimd:
                 nc.gpsimd.tensor_scalar(
-                    out=grouped[:],
-                    in0=raw.rearrange("p t c -> p c t"),
-                    scalar1=1.0,
-                    scalar2=0.0,
-                    op0=ALU.mult,
-                    op1=ALU.add,
+                    out=dst, in0=src, scalar1=1.0, scalar2=0.0, op0=ALU.mult, op1=ALU.add
                 )
             else:
-                nc.vector.tensor_copy(
-                    out=grouped[:].rearrange("p (c i) t -> p c t i", i=4),
-                    in_=raw.rearrange("p t (c i) -> p c t i", i=4),
-                )
+                nc.vector.tensor_copy(out=dst, in_=src)
             return grouped
 
         def quantise_columns(stream, q, grouped):
@@ -247,16 +240,6 @@ def tile_wavenetworklm_pa_kernel(
             )
             return gated
 
-        def multiply_by_gate_on_gpsimd(stream, g):
-            x_t = transpose_group(stream, g)
-            x_t_sb = stage.tile([P, PACK, GROUP], BF16, name="x_t_sb", bufs=2)
-            nc.scalar.copy(out=x_t_sb[:], in_=x_t[:])
-            gated = stage.tile([P, GROUP, PACK], BF16, name="gated_g", bufs=4, align_bytes=64)
-            nc.gpsimd.tensor_tensor(
-                out=gated[:], in0=x_t_sb[:].rearrange("p t w -> p w t"), in1=gate_view(g), op=ALU.mult
-            )
-            return gated
-
         def quantise_gated(stream, g, gated):
             quantise(stream["x_mx"], slice(g * GROUP, (g + 1) * GROUP), gated[:].rearrange("p w t -> p (w t)"))
 
@@ -318,17 +301,14 @@ def tile_wavenetworklm_pa_kernel(
         quantise_gated(real, 0, multiply_by_gate_on_vector(real, 0))
 
         regrouped = [regroup_columns(real, HALF_PIECES + q, True) for q in range(HALF_PIECES)]
-        gated_real = None
-        gated_imag = []
+        gated = None
         for a in range(TOKEN_TILES):
             g = a // 2
-            if a % 2 == 0:
+            if a % 2 == 0 and g + 1 < GROUPS:
+                gated = multiply_by_gate_on_vector(real, g + 1)
+            if a % 2 == 1:
                 if g + 1 < GROUPS:
-                    gated_real = multiply_by_gate_on_vector(real, g + 1)
-                gated_imag.append(multiply_by_gate_on_gpsimd(imag, g))
-            else:
-                if g + 1 < GROUPS:
-                    quantise_gated(real, g + 1, gated_real)
+                    quantise_gated(real, g + 1, gated)
                 quantise_columns(real, HALF_PIECES + g, regrouped[g])
                 spread_bias(real, HALF_PIECES + g)
             up_project_tile(real, 0, a)
@@ -337,8 +317,9 @@ def tile_wavenetworklm_pa_kernel(
         for a in range(TOKEN_TILES):
             g = a // 2
             if a % 2 == 0:
-                quantise_gated(imag, g, gated_imag[g])
+                gated = multiply_by_gate_on_vector(imag, g)
             else:
+                quantise_gated(imag, g, gated)
                 quantise_columns(imag, g, regrouped[g])
                 spread_bias(imag, g)
             up_project_tile(real, 1, a)

@@ -19,13 +19,14 @@ TOKEN_TILES = TOKENS // P
 D = 512
 F = 2048
 BANK = 512
+PSUM_BANKS = 8
 HALF = 512
 GROUP = 256
+GROUPS = TOKENS // GROUP
 STORE = 1024
 PIECE = 256
 GATE_PIECES = D // PIECE
 HALF_PIECES = STORE // PIECE
-GROUPS = TOKENS // GROUP
 RESULT_BUFS = 8
 
 FLOPS = 2 * TOKENS * D * (2 * D + 2 * F)
@@ -39,7 +40,7 @@ def tile_wavenetworklm_pa_kernel(
         keep = stack.enter_context(tc.tile_pool(name="keep", bufs=1))
         stage = stack.enter_context(tc.tile_pool(name="stage", bufs=2))
         results = stack.enter_context(tc.tile_pool(name="results", bufs=RESULT_BUFS))
-        banks = stack.enter_context(tc.psum_pool(name="banks", bufs=8))
+        banks = stack.enter_context(tc.psum_pool(name="banks", bufs=PSUM_BANKS))
         stack.enter_context(tc.manual_schedule())
 
         def mx_tiles(name, width):
@@ -56,27 +57,27 @@ def tile_wavenetworklm_pa_kernel(
         gate = keep.tile([P, PACK, TOKENS], F32, name="gate")
 
         amplitude = {
-            "x": keep.tile([P, TOKEN_TILES * D], BF16, name="amp_sb"),
             "x_dram": amp,
+            "x": keep.tile([P, TOKEN_TILES * D], BF16, name="amp_sb"),
             "x_mx": mx_tiles("amp", TOKENS),
-            "w_raw": keep.tile([P, PACK, D], BF16, name="wa_raw"),
             "w_dram": Wa,
+            "w_raw": keep.tile([P, PACK, D], BF16, name="wa_raw"),
             "w_mx": mx_tiles("wa", D),
         }
         phase = {
-            "x": keep.tile([P, TOKEN_TILES * D], BF16, name="ph_sb"),
             "x_dram": ph,
+            "x": keep.tile([P, TOKEN_TILES * D], BF16, name="ph_sb"),
             "x_mx": mx_tiles("ph", TOKENS),
-            "w_raw": keep.tile([P, PACK, D], BF16, name="wp_raw"),
             "w_dram": Wp,
+            "w_raw": keep.tile([P, PACK, D], BF16, name="wp_raw"),
             "w_mx": mx_tiles("wp", D),
         }
         real = {
-            "x": keep.tile([P, TOKEN_TILES * D], BF16, name="cr_sb"),
             "x_dram": cr,
+            "x": keep.tile([P, TOKEN_TILES * D], BF16, name="cr_sb"),
             "x_mx": mx_tiles("gr", TOKENS),
-            "w_raw": keep.tile([P, PACK, F], BF16, name="w1r_raw"),
             "w_dram": w1r,
+            "w_raw": keep.tile([P, PACK, F], BF16, name="w1r_raw"),
             "w_mx": mx_tiles("w1r", F),
             "bias_dram": b1r,
             "bias_row": 0,
@@ -84,11 +85,11 @@ def tile_wavenetworklm_pa_kernel(
             "out": out_0.flatten_outer_dims().rearrange("(p a) f -> p a f", a=TOKEN_TILES),
         }
         imag = {
-            "x": keep.tile([P, TOKEN_TILES * D], BF16, name="ci_sb"),
             "x_dram": ci,
+            "x": keep.tile([P, TOKEN_TILES * D], BF16, name="ci_sb"),
             "x_mx": mx_tiles("gi", TOKENS),
-            "w_raw": keep.tile([P, PACK, F], BF16, name="w1i_raw"),
             "w_dram": w1i,
+            "w_raw": keep.tile([P, PACK, F], BF16, name="w1i_raw"),
             "w_mx": mx_tiles("w1i", F),
             "bias_dram": b1i,
             "bias_row": 1,
@@ -144,37 +145,41 @@ def tile_wavenetworklm_pa_kernel(
                 stop=stop,
             )
 
-        def regroup_columns(stream, q, on_gpsimd):
-            grouped = stage.tile([P, PIECE, PACK], BF16, name="w_grouped", bufs=4, align_bytes=64)
+        def regroup_columns(stream, q, engine):
+            grouped = stage.tile(
+                [P, PIECE, PACK], BF16, name="w_grouped", bufs=2 * HALF_PIECES, align_bytes=64
+            )
             dst = grouped[:].rearrange("p (c i) t -> p c t i", i=4)
             src = stream["w_raw"][:, :, q * PIECE : (q + 1) * PIECE].rearrange("p t (c i) -> p c t i", i=4)
-            if on_gpsimd:
+            if engine == "vector":
+                nc.vector.tensor_copy(out=dst, in_=src)
+            elif engine == "scalar":
+                nc.scalar.copy(out=dst, in_=src)
+            else:
                 nc.gpsimd.tensor_scalar(
                     out=dst, in0=src, scalar1=1.0, scalar2=0.0, op0=ALU.mult, op1=ALU.add
                 )
-            else:
-                nc.vector.tensor_copy(out=dst, in_=src)
             return grouped
 
         def quantise_columns(stream, q, grouped):
             quantise(stream["w_mx"], slice(q * PIECE, (q + 1) * PIECE), grouped[:].rearrange("p c t -> p (c t)"))
 
-        def spread_bias(stream, q):
-            cols = slice(q * PIECE, (q + 1) * PIECE)
+        def spread_bias(stream, s):
             j = stream["bias_row"]
-            spread_ps = banks.tile([P, PIECE], F32, name="spread_ps", tag="bank")
-            nc.tensor.matmul(
-                out=spread_ps[:],
-                lhsT=ident_bf16[:, j : j + 1].to_broadcast([P, P]),
-                rhs=up_bias_rows[:, cols],
-                start=True,
-                stop=True,
-            )
-            nc.scalar.copy(out=stream["bias"][:, cols], in_=spread_ps[:])
+            spread_ps = banks.tile([P, STORE], BF16, name="spread_ps", tag="bank")
+            for c in range(STORE // BANK):
+                nc.tensor.matmul(
+                    out=spread_ps[:, c * BANK : (c + 1) * BANK],
+                    lhsT=ident_bf16[:, j : j + 1].to_broadcast([P, P]),
+                    rhs=up_bias_rows[:, s * STORE + c * BANK : s * STORE + (c + 1) * BANK],
+                    start=True,
+                    stop=True,
+                )
+            nc.scalar.copy(out=stream["bias"][:, s * STORE : (s + 1) * STORE], in_=spread_ps[:])
 
         def quantise_token_half(stream, h):
             x_words = stream["x"][:].bitcast(F32)
-            grouped = stage.tile([P, HALF * PACK], BF16, name="x_grouped", bufs=4, align_bytes=64)
+            grouped = stage.tile([P, HALF * PACK], BF16, name="x_grouped", align_bytes=64)
             grouped_words = grouped[:].bitcast(F32).rearrange("p (w u) -> p w u", u=2)
             for g in range(HALF // GROUP):
                 words_t = banks.tile([P, 2, GROUP], F32, name="words_t", tag="bank")
@@ -234,9 +239,19 @@ def tile_wavenetworklm_pa_kernel(
 
         def multiply_by_gate_on_vector(stream, g):
             x_t = transpose_group(stream, g)
-            gated = stage.tile([P, GROUP, PACK], BF16, name="gated_v", bufs=2, align_bytes=64)
+            gated = stage.tile([P, GROUP, PACK], BF16, name="gated_v", align_bytes=64)
             nc.vector.tensor_tensor(
                 out=gated[:], in0=x_t[:].rearrange("p t w -> p w t"), in1=gate_view(g), op=ALU.mult
+            )
+            return gated
+
+        def multiply_by_gate_on_gpsimd(stream, g):
+            x_t = transpose_group(stream, g)
+            x_t_sb = stage.tile([P, PACK, GROUP], BF16, name="x_t_sb", bufs=GROUPS)
+            nc.scalar.copy(out=x_t_sb[:], in_=x_t[:])
+            gated = stage.tile([P, GROUP, PACK], BF16, name="gated_g", bufs=GROUPS, align_bytes=64)
+            nc.gpsimd.tensor_tensor(
+                out=gated[:], in0=x_t_sb[:].rearrange("p t w -> p w t"), in1=gate_view(g), op=ALU.mult
             )
             return gated
 
@@ -265,6 +280,7 @@ def tile_wavenetworklm_pa_kernel(
         nc.vector.memset(gate_bias_rows[:], 0.0)
         nc.vector.memset(up_bias_rows[:], 0.0)
         nc.scalar.activation(out=warm[:], in_=warm[:], func=ACT.Sigmoid)
+
         load_gate_weight(amplitude)
         load_gate_weight(phase)
         load_gate_biases()
@@ -282,53 +298,58 @@ def tile_wavenetworklm_pa_kernel(
         load_token_half(imag, 1)
         load_up_weight_half(imag, 0)
         load_up_weight_half(imag, 1)
-        regrouped = [regroup_columns(w, q, False) for w in (amplitude, phase) for q in range(GATE_PIECES)]
+
+        regrouped = [regroup_columns(w, q, "vector") for w in (amplitude, phase) for q in range(GATE_PIECES)]
         for i, w in enumerate((amplitude, phase)):
             for q in range(GATE_PIECES):
                 quantise_columns(w, q, regrouped[i * GATE_PIECES + q])
-        quantise_token_half(amplitude, 0)
-        quantise_token_half(phase, 0)
-        quantise_token_half(amplitude, 1)
-        quantise_token_half(phase, 1)
+        for h in range(TOKENS // HALF):
+            quantise_token_half(amplitude, h)
+            quantise_token_half(phase, h)
         sum_gate_biases()
-        gate_half(0)
-        gate_half(1)
-        regrouped = [regroup_columns(real, q, False) for q in range(HALF_PIECES)]
+        for h in range(TOKENS // HALF):
+            gate_half(h)
+
+        regrouped = [regroup_columns(real, q, "vector") for q in range(HALF_PIECES)]
         for q in range(HALF_PIECES):
             quantise_columns(real, q, regrouped[q])
-        for q in range(HALF_PIECES):
-            spread_bias(real, q)
+        spread_bias(real, 0)
         quantise_gated(real, 0, multiply_by_gate_on_vector(real, 0))
 
-        regrouped = [regroup_columns(real, HALF_PIECES + q, True) for q in range(HALF_PIECES)]
-        gated = None
-        for a in range(TOKEN_TILES):
-            g = a // 2
-            if a % 2 == 0 and g + 1 < GROUPS:
-                gated = multiply_by_gate_on_vector(real, g + 1)
-            if a % 2 == 1:
-                if g + 1 < GROUPS:
-                    quantise_gated(real, g + 1, gated)
-                quantise_columns(real, HALF_PIECES + g, regrouped[g])
-                spread_bias(real, HALF_PIECES + g)
-            up_project_tile(real, 0, a)
 
-        regrouped = [regroup_columns(imag, q, True) for q in range(HALF_PIECES)]
+        spread_bias(real, 1)
+        regrouped = []
+        gated_real = None
+        gated_imag = []
         for a in range(TOKEN_TILES):
             g = a // 2
             if a % 2 == 0:
-                gated = multiply_by_gate_on_vector(imag, g)
+                if g + 1 < GROUPS:
+                    gated_real = multiply_by_gate_on_vector(real, g + 1)
+                gated_imag.append(multiply_by_gate_on_gpsimd(imag, g))
+            elif g + 1 < GROUPS:
+                quantise_gated(real, g + 1, gated_real)
+            if a < HALF_PIECES:
+                regrouped.append(regroup_columns(real, HALF_PIECES + a, "scalar"))
             else:
-                quantise_gated(imag, g, gated)
-                quantise_columns(imag, g, regrouped[g])
-                spread_bias(imag, g)
+                quantise_columns(real, a, regrouped[a - HALF_PIECES])
+            up_project_tile(real, 0, a)
+
+        spread_bias(imag, 0)
+        regrouped = []
+        regrouped_late = [regroup_columns(imag, HALF_PIECES + q, "gpsimd") for q in range(HALF_PIECES)]
+        for a in range(TOKEN_TILES):
+            if a < HALF_PIECES:
+                quantise_gated(imag, a, gated_imag[a])
+                regrouped.append(regroup_columns(imag, a, "scalar"))
+            else:
+                quantise_columns(imag, a - HALF_PIECES, regrouped[a - HALF_PIECES])
             up_project_tile(real, 1, a)
 
-        regrouped = [regroup_columns(imag, HALF_PIECES + q, True) for q in range(HALF_PIECES)]
+        spread_bias(imag, 1)
         for a in range(TOKEN_TILES):
             if a % 2 == 1:
-                quantise_columns(imag, HALF_PIECES + a // 2, regrouped[a // 2])
-                spread_bias(imag, HALF_PIECES + a // 2)
+                quantise_columns(imag, HALF_PIECES + a // 2, regrouped_late[a // 2])
             up_project_tile(imag, 0, a)
 
         for a in range(TOKEN_TILES):

@@ -234,24 +234,14 @@ def tile_wavenetworklm_pa_kernel(
                     )
             return x_t
 
-        def gate_view(g):
-            return gate[:, :, g * GROUP : (g + 1) * GROUP].rearrange("p t w -> p w t")
-
-        def multiply_by_gate_on_vector(stream, g):
+        def multiply_by_gate(stream, g):
             x_t = transpose_group(stream, g)
-            gated = stage.tile([P, GROUP, PACK], BF16, name="gated_v", align_bytes=64)
+            gated = stage.tile([P, GROUP, PACK], BF16, name="gated", align_bytes=64)
             nc.vector.tensor_tensor(
-                out=gated[:], in0=x_t[:].rearrange("p t w -> p w t"), in1=gate_view(g), op=ALU.mult
-            )
-            return gated
-
-        def multiply_by_gate_on_gpsimd(stream, g):
-            x_t = transpose_group(stream, g)
-            x_t_sb = stage.tile([P, PACK, GROUP], BF16, name="x_t_sb", bufs=GROUPS)
-            nc.scalar.copy(out=x_t_sb[:], in_=x_t[:])
-            gated = stage.tile([P, GROUP, PACK], BF16, name="gated_g", bufs=GROUPS, align_bytes=64)
-            nc.gpsimd.tensor_tensor(
-                out=gated[:], in0=x_t_sb[:].rearrange("p t w -> p w t"), in1=gate_view(g), op=ALU.mult
+                out=gated[:],
+                in0=x_t[:].rearrange("p t w -> p w t"),
+                in1=gate[:, :, g * GROUP : (g + 1) * GROUP].rearrange("p t w -> p w t"),
+                op=ALU.mult,
             )
             return gated
 
@@ -314,21 +304,18 @@ def tile_wavenetworklm_pa_kernel(
         for q in range(HALF_PIECES):
             quantise_columns(real, q, regrouped[q])
         spread_bias(real, 0)
-        quantise_gated(real, 0, multiply_by_gate_on_vector(real, 0))
+        quantise_gated(real, 0, multiply_by_gate(real, 0))
 
 
         spread_bias(real, 1)
         regrouped = []
-        gated_real = None
-        gated_imag = []
+        gated = None
         for a in range(TOKEN_TILES):
-            g = a // 2
-            if a % 2 == 0:
-                if g + 1 < GROUPS:
-                    gated_real = multiply_by_gate_on_vector(real, g + 1)
-                gated_imag.append(multiply_by_gate_on_gpsimd(imag, g))
-            elif g + 1 < GROUPS:
-                quantise_gated(real, g + 1, gated_real)
+            g = a // 2 + 1
+            if a % 2 == 0 and g < GROUPS:
+                gated = multiply_by_gate(real, g)
+            if a % 2 == 1 and g < GROUPS:
+                quantise_gated(real, g, gated)
             if a < HALF_PIECES:
                 regrouped.append(regroup_columns(real, HALF_PIECES + a, "scalar"))
             else:
@@ -339,8 +326,11 @@ def tile_wavenetworklm_pa_kernel(
         regrouped = []
         regrouped_late = [regroup_columns(imag, HALF_PIECES + q, "gpsimd") for q in range(HALF_PIECES)]
         for a in range(TOKEN_TILES):
+            if a % 2 == 0:
+                gated = multiply_by_gate(imag, a // 2)
+            else:
+                quantise_gated(imag, a // 2, gated)
             if a < HALF_PIECES:
-                quantise_gated(imag, a, gated_imag[a])
                 regrouped.append(regroup_columns(imag, a, "scalar"))
             else:
                 quantise_columns(imag, a - HALF_PIECES, regrouped[a - HALF_PIECES])

@@ -238,9 +238,9 @@ def tile_wavenetworklm_pa_kernel(
             x_t = transpose_group(stream, g)
             gated = stage.tile([P, GROUP, PACK], BF16, name="gated", align_bytes=64)
             nc.vector.tensor_tensor(
-                out=gated[:],
-                in0=x_t[:].rearrange("p t w -> p w t"),
-                in1=gate[:, :, g * GROUP : (g + 1) * GROUP].rearrange("p t w -> p w t"),
+                out=gated[:].rearrange("p (c i) t -> p c t i", i=4),
+                in0=x_t[:].rearrange("p t (c i) -> p c t i", i=4),
+                in1=gate[:, :, g * GROUP : (g + 1) * GROUP].rearrange("p t (c i) -> p c t i", i=4),
                 op=ALU.mult,
             )
             return gated

@@ -149,8 +149,8 @@ def tile_wavenetworklm_pa_kernel(
             grouped = stage.tile(
                 [P, PIECE, PACK], BF16, name="w_grouped", bufs=2 * HALF_PIECES, align_bytes=64
             )
-            dst = grouped[:].rearrange("p (c i) t -> p c t i", i=4)
-            src = stream["w_raw"][:, :, q * PIECE : (q + 1) * PIECE].rearrange("p t (c i) -> p c t i", i=4)
+            dst = grouped[:].rearrange("p (c i) t -> p c t i", i=8)
+            src = stream["w_raw"][:, :, q * PIECE : (q + 1) * PIECE].rearrange("p t (c i) -> p c t i", i=8)
             if engine == "vector":
                 nc.vector.tensor_copy(out=dst, in_=src)
             elif engine == "scalar":
@@ -234,8 +234,9 @@ def tile_wavenetworklm_pa_kernel(
                     )
             return x_t
 
-        def multiply_by_gate(stream, g):
-            x_t = transpose_group(stream, g)
+        def multiply_by_gate(stream, g, x_t=None):
+            if x_t is None:
+                x_t = transpose_group(stream, g)
             gated = stage.tile([P, GROUP, PACK], BF16, name="gated", align_bytes=64)
             nc.vector.tensor_tensor(
                 out=gated[:].rearrange("p (c i) t -> p c t i", i=4),
@@ -293,18 +294,23 @@ def tile_wavenetworklm_pa_kernel(
         for i, w in enumerate((amplitude, phase)):
             for q in range(GATE_PIECES):
                 quantise_columns(w, q, regrouped[i * GATE_PIECES + q])
+        sum_gate_biases()
         for h in range(TOKENS // HALF):
             quantise_token_half(amplitude, h)
             quantise_token_half(phase, h)
-        sum_gate_biases()
-        for h in range(TOKENS // HALF):
-            gate_half(h)
+        gate_half(0)
+        x_t = [transpose_group(real, g) for g in range(2)]
+        regrouped_early = [regroup_columns(real, q, "scalar") for q in range(HALF_PIECES - 1, HALF_PIECES)]
+        gate_half(1)
 
-        regrouped = [regroup_columns(real, q, "vector") for q in range(HALF_PIECES)]
-        for q in range(HALF_PIECES):
-            quantise_columns(real, q, regrouped[q])
+        regrouped = [regroup_columns(real, q, "vector") for q in range(HALF_PIECES - 1)]
         spread_bias(real, 0)
-        quantise_gated(real, 0, multiply_by_gate(real, 0))
+        for q in range(HALF_PIECES - 1):
+            quantise_columns(real, q, regrouped[q])
+        gated = multiply_by_gate(real, 0, x_t[0])
+        for q in range(HALF_PIECES - 1, HALF_PIECES):
+            quantise_columns(real, q, regrouped_early[q - (HALF_PIECES - 1)])
+        quantise_gated(real, 0, gated)
 
 
         spread_bias(real, 1)
@@ -313,7 +319,7 @@ def tile_wavenetworklm_pa_kernel(
         for a in range(TOKEN_TILES):
             g = a // 2 + 1
             if a % 2 == 0 and g < GROUPS:
-                gated = multiply_by_gate(real, g)
+                gated = multiply_by_gate(real, g, x_t[g] if g < len(x_t) else None)
             if a % 2 == 1 and g < GROUPS:
                 quantise_gated(real, g, gated)
             if a < HALF_PIECES:

from contextlib import ExitStack

import concourse.mybir as mybir
from concourse.masks import make_identity

F32 = mybir.dt.float32
BF16 = mybir.dt.bfloat16
U32 = mybir.dt.uint32
U8 = mybir.dt.uint8
FP8X4 = mybir.dt.float8_e4m3fn_x4
ACT = mybir.ActivationFunctionType
ALU = mybir.AluOpType
AXIS = mybir.AxisListType

P = 128
PACK = 4
TOKENS = 1024
TOKEN_TILES = TOKENS // P
D = 512
F = 2048
BANK = 512
PSUM_BANKS = 8
HALF = 512
GROUP = 256
GROUPS = TOKENS // GROUP
STORE = 1024
PIECE = 256
GATE_PIECES = D // PIECE
HALF_PIECES = STORE // PIECE
RESULT_BUFS = 8

FLOPS = 2 * TOKENS * D * (2 * D + 2 * F)


def tile_wavenetworklm_pa_kernel(
    tc, amp, ph, cr, ci, Wa, ba, Wp, bp, gate_bias, w1r, b1r, w1i, b1i, out_0, out_1
):
    nc = tc.nc
    with ExitStack() as stack:
        keep = stack.enter_context(tc.tile_pool(name="keep", bufs=1))
        stage = stack.enter_context(tc.tile_pool(name="stage", bufs=2))
        results = stack.enter_context(tc.tile_pool(name="results", bufs=RESULT_BUFS))
        banks = stack.enter_context(tc.psum_pool(name="banks", bufs=PSUM_BANKS))
        stack.enter_context(tc.manual_schedule())

        def mx_tiles(name, width):
            codes = keep.tile([P, width], U32, name=name + "_codes", align_bytes=64)
            scales = keep.tile([P, width], U8, name=name + "_scales", align_bytes=64)
            return codes, scales

        ident_f32 = keep.tile([P, P], F32, name="ident_f32")
        ident_bf16 = keep.tile([P, P], BF16, name="ident_bf16")
        gate_bias_rows = keep.tile([P, P], BF16, name="gate_bias_rows")
        up_bias_rows = keep.tile([P, F], BF16, name="up_bias_rows")
        warm = keep.tile([P, 1], F32, name="warm")
        gate_shift = keep.tile([P, PACK], F32, name="gate_shift")
        gate = keep.tile([P, PACK, TOKENS], F32, name="gate")

        amplitude = {
            "x_dram": amp,
            "x": keep.tile([P, TOKEN_TILES * D], BF16, name="amp_sb"),
            "x_mx": mx_tiles("amp", TOKENS),
            "w_dram": Wa,
            "w_raw": keep.tile([P, PACK, D], BF16, name="wa_raw"),
            "w_mx": mx_tiles("wa", D),
        }
        phase = {
            "x_dram": ph,
            "x": keep.tile([P, TOKEN_TILES * D], BF16, name="ph_sb"),
            "x_mx": mx_tiles("ph", TOKENS),
            "w_dram": Wp,
            "w_raw": keep.tile([P, PACK, D], BF16, name="wp_raw"),
            "w_mx": mx_tiles("wp", D),
        }
        real = {
            "x_dram": cr,
            "x": keep.tile([P, TOKEN_TILES * D], BF16, name="cr_sb"),
            "x_mx": mx_tiles("gr", TOKENS),
            "w_dram": w1r,
            "w_raw": keep.tile([P, PACK, F], BF16, name="w1r_raw"),
            "w_mx": mx_tiles("w1r", F),
            "bias_dram": b1r,
            "bias_row": 0,
            "bias": keep.tile([P, F], BF16, name="b1r_spread"),
            "out": out_0.flatten_outer_dims().rearrange("(p a) f -> p a f", a=TOKEN_TILES),
        }
        imag = {
            "x_dram": ci,
            "x": keep.tile([P, TOKEN_TILES * D], BF16, name="ci_sb"),
            "x_mx": mx_tiles("gi", TOKENS),
            "w_dram": w1i,
            "w_raw": keep.tile([P, PACK, F], BF16, name="w1i_raw"),
            "w_mx": mx_tiles("w1i", F),
            "bias_dram": b1i,
            "bias_row": 1,
            "bias": keep.tile([P, F], BF16, name="b1i_spread"),
            "out": out_1.flatten_outer_dims().rearrange("(p a) f -> p a f", a=TOKEN_TILES),
        }

        def load_token_half(stream, h):
            cols = slice(h * HALF // P * D, (h + 1) * HALF // P * D)
            x_view = stream["x_dram"].flatten_outer_dims().rearrange("(p a) c -> p (a c)", a=TOKEN_TILES)
            nc.sync.dma_start(out=stream["x"][:, cols], in_=x_view[:, cols])

        def load_gate_weight(stream):
            nc.sync.dma_start(
                out=stream["w_raw"][:].rearrange("p (u e) n -> p u e n", e=2),
                in_=stream["w_dram"].rearrange("(u p e) n -> p u e n", u=2, e=2),
            )

        def load_up_weight_half(stream, s):
            cols = slice(s * STORE, (s + 1) * STORE)
            nc.sync.dma_start(
                out=stream["w_raw"][:, :, cols],
                in_=stream["w_dram"].rearrange("(t p) n -> p t n", p=P)[:, :, cols],
            )

        def load_gate_biases():
            for j, vec in enumerate((ba, bp, gate_bias)):
                nc.sync.dma_start(
                    out=gate_bias_rows[PACK * j : PACK * (j + 1), :],
                    in_=vec.rearrange("(m p) -> m p", p=P),
                )

        def load_up_bias(stream):
            j = stream["bias_row"]
            nc.sync.dma_start(
                out=up_bias_rows[j : j + 1, :], in_=stream["bias_dram"].rearrange("(o f) -> o f", o=1)
            )

        def quantise(mx, cols, grouped):
            codes, scales = mx
            nc.vector.quantize_mx(
                out=codes[:, cols].bitcast(FP8X4), scales=scales[:, cols], in_=grouped
            )

        def multiply_mx(out, stationary, rows, moving, cols, start, stop):
            nc.tensor.matmul_mx(
                out=out,
                lhsT=stationary[0][:, rows].bitcast(FP8X4),
                lhsT_scale=stationary[1][:, rows],
                rhs=moving[0][:, cols].bitcast(FP8X4),
                rhs_scale=moving[1][:, cols],
                start=start,
                stop=stop,
            )

        def regroup_columns(stream, q, engine):
            grouped = stage.tile(
                [P, PIECE, PACK], BF16, name="w_grouped", bufs=2 * HALF_PIECES, align_bytes=64
            )
            dst = grouped[:].rearrange("p (c i) t -> p c t i", i=8)
            src = stream["w_raw"][:, :, q * PIECE : (q + 1) * PIECE].rearrange("p t (c i) -> p c t i", i=8)
            if engine == "vector":
                nc.vector.tensor_copy(out=dst, in_=src)
            elif engine == "scalar":
                nc.scalar.copy(out=dst, in_=src)
            else:
                nc.gpsimd.tensor_scalar(
                    out=dst, in0=src, scalar1=1.0, scalar2=0.0, op0=ALU.mult, op1=ALU.add
                )
            return grouped

        def quantise_columns(stream, q, grouped):
            quantise(stream["w_mx"], slice(q * PIECE, (q + 1) * PIECE), grouped[:].rearrange("p c t -> p (c t)"))

        def spread_bias(stream, s):
            j = stream["bias_row"]
            spread_ps = banks.tile([P, STORE], BF16, name="spread_ps", tag="bank")
            for c in range(STORE // BANK):
                nc.tensor.matmul(
                    out=spread_ps[:, c * BANK : (c + 1) * BANK],
                    lhsT=ident_bf16[:, j : j + 1].to_broadcast([P, P]),
                    rhs=up_bias_rows[:, s * STORE + c * BANK : s * STORE + (c + 1) * BANK],
                    start=True,
                    stop=True,
                )
            nc.scalar.copy(out=stream["bias"][:, s * STORE : (s + 1) * STORE], in_=spread_ps[:])

        def quantise_token_half(stream, h):
            x_words = stream["x"][:].bitcast(F32)
            grouped = stage.tile([P, HALF * PACK], BF16, name="x_grouped", align_bytes=64)
            grouped_words = grouped[:].bitcast(F32).rearrange("p (w u) -> p w u", u=2)
            for g in range(HALF // GROUP):
                words_t = banks.tile([P, 2, GROUP], F32, name="words_t", tag="bank")
                for j in range(GROUP // P):
                    a = (h * HALF + g * GROUP) // P + j
                    for u in range(2):
                        first = a * (D // 2) + u * P
                        nc.tensor.transpose(
                            out=words_t[:, u, j * P : (j + 1) * P],
                            in_=x_words[:, first : first + P],
                            identity=ident_f32[:],
                        )
                nc.scalar.copy(
                    out=grouped_words[:, g * GROUP : (g + 1) * GROUP, :],
                    in_=words_t[:].rearrange("p u w -> p w u"),
                )
            quantise(stream["x_mx"], slice(h * HALF, (h + 1) * HALF), grouped[:])

        def sum_gate_biases():
            bias_cols_ps = banks.tile([P, P], BF16, name="bias_cols_ps", tag="bank")
            nc.tensor.transpose(out=bias_cols_ps[:], in_=gate_bias_rows[:], identity=ident_bf16[:])
            bias_cols = keep.tile([P, 3 * PACK], F32, name="bias_cols")
            nc.vector.tensor_copy(out=bias_cols[:], in_=bias_cols_ps[:, 0 : 3 * PACK])
            nc.vector.tensor_reduce(
                out=gate_shift[:],
                in_=bias_cols[:].rearrange("p (j m) -> p m j", m=PACK),
                axis=AXIS.X,
                op=ALU.add,
            )

        def gate_half(h):
            cols = slice(h * HALF, (h + 1) * HALF)
            for m in range(PACK):
                rows = slice(m * P, (m + 1) * P)
                z = banks.tile([P, HALF], F32, name="z", tag="bank")
                multiply_mx(z[:], amplitude["w_mx"], rows, amplitude["x_mx"], cols, True, False)
                multiply_mx(z[:], phase["w_mx"], rows, phase["x_mx"], cols, False, True)
                nc.scalar.activation(
                    out=gate[:, m, cols], in_=z[:], func=ACT.Sigmoid, bias=gate_shift[:, m : m + 1]
                )

        def transpose_group(stream, g):
            x_t = banks.tile([P, PACK, GROUP], BF16, name="x_t", tag="bank")
            for j in range(GROUP // P):
                a = g * GROUP // P + j
                for t in range(PACK):
                    first = a * D + t * P
                    nc.tensor.transpose(
                        out=x_t[:, t, j * P : (j + 1) * P],
                        in_=stream["x"][:, first : first + P],
                        identity=ident_bf16[:],
                    )
            return x_t

        def multiply_by_gate(stream, g, x_t=None):
            if x_t is None:
                x_t = transpose_group(stream, g)
            gated = stage.tile([P, GROUP, PACK], BF16, name="gated", align_bytes=64)
            nc.vector.tensor_tensor(
                out=gated[:].rearrange("p (c i) t -> p c t i", i=4),
                in0=x_t[:].rearrange("p t (c i) -> p c t i", i=4),
                in1=gate[:, :, g * GROUP : (g + 1) * GROUP].rearrange("p t (c i) -> p c t i", i=4),
                op=ALU.mult,
            )
            return gated

        def quantise_gated(stream, g, gated):
            quantise(stream["x_mx"], slice(g * GROUP, (g + 1) * GROUP), gated[:].rearrange("p w t -> p (w t)"))

        def up_project_tile(stream, s, a):
            rows = slice(a * P, (a + 1) * P)
            result = results.tile([P, STORE], F32, name="result")
            for c in range(STORE // BANK):
                cols = slice(s * STORE + c * BANK, s * STORE + (c + 1) * BANK)
                acc = banks.tile([P, BANK], F32, name="acc", tag="bank")
                multiply_mx(acc[:], stream["x_mx"], rows, stream["w_mx"], cols, True, True)
                nc.vector.tensor_tensor(
                    out=result[:, c * BANK : (c + 1) * BANK],
                    in0=acc[:],
                    in1=stream["bias"][:, cols],
                    op=ALU.add,
                )
            nc.scalar.activation(out=result[:], in_=result[:], func=ACT.Gelu)
            nc.sync.dma_start(out=stream["out"][:, a, s * STORE : (s + 1) * STORE], in_=result[:])

        make_identity(nc, ident_f32[:])
        make_identity(nc, ident_bf16[:])
        nc.vector.memset(warm[:], 0.0)
        nc.vector.memset(gate_bias_rows[:], 0.0)
        nc.vector.memset(up_bias_rows[:], 0.0)
        nc.scalar.activation(out=warm[:], in_=warm[:], func=ACT.Sigmoid)

        load_gate_weight(amplitude)
        load_gate_weight(phase)
        load_gate_biases()
        load_token_half(amplitude, 0)
        load_token_half(phase, 0)
        load_token_half(amplitude, 1)
        load_token_half(phase, 1)
        load_up_bias(real)
        load_up_bias(imag)
        load_up_weight_half(real, 0)
        load_token_half(real, 0)
        load_token_half(real, 1)
        load_up_weight_half(real, 1)
        load_token_half(imag, 0)
        load_token_half(imag, 1)
        load_up_weight_half(imag, 0)
        load_up_weight_half(imag, 1)

        regrouped = [regroup_columns(w, q, "vector") for w in (amplitude, phase) for q in range(GATE_PIECES)]
        for i, w in enumerate((amplitude, phase)):
            for q in range(GATE_PIECES):
                quantise_columns(w, q, regrouped[i * GATE_PIECES + q])
        sum_gate_biases()
        for h in range(TOKENS // HALF):
            quantise_token_half(amplitude, h)
            quantise_token_half(phase, h)
        gate_half(0)
        x_t = [transpose_group(real, g) for g in range(2)]
        regrouped_early = [regroup_columns(real, q, "scalar") for q in range(HALF_PIECES - 1, HALF_PIECES)]
        gate_half(1)

        regrouped = [regroup_columns(real, q, "vector") for q in range(HALF_PIECES - 1)]
        spread_bias(real, 0)
        for q in range(HALF_PIECES - 1):
            quantise_columns(real, q, regrouped[q])
        gated = multiply_by_gate(real, 0, x_t[0])
        for q in range(HALF_PIECES - 1, HALF_PIECES):
            quantise_columns(real, q, regrouped_early[q - (HALF_PIECES - 1)])
        quantise_gated(real, 0, gated)


        spread_bias(real, 1)
        regrouped = []
        gated = None
        for a in range(TOKEN_TILES):
            g = a // 2 + 1
            if a % 2 == 0 and g < GROUPS:
                gated = multiply_by_gate(real, g, x_t[g] if g < len(x_t) else None)
            if a % 2 == 1 and g < GROUPS:
                quantise_gated(real, g, gated)
            if a < HALF_PIECES:
                regrouped.append(regroup_columns(real, HALF_PIECES + a, "scalar"))
            else:
                quantise_columns(real, a, regrouped[a - HALF_PIECES])
            up_project_tile(real, 0, a)

        spread_bias(imag, 0)
        regrouped = []
        regrouped_late = [regroup_columns(imag, HALF_PIECES + q, "gpsimd") for q in range(HALF_PIECES)]
        for a in range(TOKEN_TILES):
            if a % 2 == 0:
                gated = multiply_by_gate(imag, a // 2)
            else:
                quantise_gated(imag, a // 2, gated)
            if a < HALF_PIECES:
                regrouped.append(regroup_columns(imag, a, "scalar"))
            else:
                quantise_columns(imag, a - HALF_PIECES, regrouped[a - HALF_PIECES])
            up_project_tile(real, 1, a)

        spread_bias(imag, 1)
        for a in range(TOKEN_TILES):
            if a % 2 == 1:
                quantise_columns(imag, HALF_PIECES + a // 2, regrouped_late[a // 2])
            up_project_tile(imag, 0, a)

        for a in range(TOKEN_TILES):
            up_project_tile(imag, 1, a)
